import numpy as np
import ml_dtypes


def mxq(x, axis, fmt="e4m3"):
    dtype, down = {"e4m3": (ml_dtypes.float8_e4m3fn, 7), "e5m2": (ml_dtypes.float8_e5m2, 14)}[fmt]
    v = np.moveaxis(np.asarray(x, np.float32).astype(ml_dtypes.bfloat16).astype(np.float64), axis, -1)
    blocks = v.reshape(v.shape[:-1] + (-1, 32))
    amax = np.abs(blocks).max(-1, keepdims=True)
    byte = np.maximum(np.where(amax > 0, np.frexp(amax)[1] - 1 + 127, 0) - down, 1)
    scale = np.exp2(byte - 127.0)
    codes = (blocks / scale).astype(np.float32).astype(dtype).astype(np.float64)
    return np.moveaxis((codes * scale).reshape(v.shape), -1, axis)


WIDE = False


def mx_kscale(k):
    if not WIDE:
        return np.ones(k)
    levels = np.array([10, -10, 5, -5, 0])
    a = np.random.permutation(np.resize(levels, k // 512 * 4)).reshape(k // 512, 4)
    idx = np.arange(k)
    return np.exp2(a[idx // 512, idx % 128 // 32])


BF16 = ml_dtypes.bfloat16


def bf(x):
    return np.asarray(x, np.float32).astype(BF16)


def f64(x):
    return np.asarray(x).astype(np.float64)


B, S, D, H, HKV, DH, QB = 2, 2048, 1024, 2, 1, 128, 512
THETA = 1000000.0


def rotate_half(u):
    return np.stack((-u[..., 1::2], u[..., ::2]), axis=-1).reshape(u.shape)


def setup_inputs():
    s = mx_kscale(D)
    inv_freq = 1.0 / THETA ** (np.arange(0, DH, 2) / DH)
    emb = np.repeat(np.outer(np.arange(S), inv_freq), 2, axis=-1)
    return {"x": bf(np.random.standard_normal((B, S, D)) * s),
            "cos": bf(np.cos(emb)),
            "sin": bf(np.sin(emb)),
            "Wq": bf(np.random.standard_normal((D, H * DH)) * 1.5 / np.sqrt(D) / s[:, None]),
            "Wk": bf(np.random.standard_normal((D, HKV * DH)) * 1.5 / np.sqrt(D) / s[:, None]),
            "Wv": bf(np.random.standard_normal((D, HKV * DH)) / np.sqrt(D) / s[:, None])}


def reference(x, cos, sin, Wq, Wk, Wv):
    xq = mxq(f64(x), 2, "e4m3")
    q = (xq @ mxq(f64(Wq), 0, "e4m3")).reshape(B, S, H, DH).transpose(0, 2, 1, 3)
    k = (xq @ mxq(f64(Wk), 0, "e4m3")).reshape(B, S, HKV, DH).transpose(0, 2, 1, 3)
    v = (xq @ mxq(f64(Wv), 0, "e4m3")).reshape(B, S, HKV, DH).transpose(0, 2, 1, 3)
    c = f64(cos)[None, None, :, :]
    sn = f64(sin)[None, None, :, :]
    q = q * c + rotate_half(q) * sn
    k = k * c + rotate_half(k) * sn
    return q, k, v

@@ -1,0 +1,217 @@
+from contextlib import ExitStack
+
+import concourse.mybir as mybir
+from concourse.masks import make_identity
+
+F32 = mybir.dt.float32
+BF16 = mybir.dt.bfloat16
+U32 = mybir.dt.uint32
+U8 = mybir.dt.uint8
+FP8X4 = mybir.dt.float8_e4m3fn_x4
+MULT = mybir.AluOpType.mult
+ADD = mybir.AluOpType.add
+
+P = 128
+BATCH = 2
+SEQ = 2048
+DIM = 1024
+HEAD = 128
+ROTATED = 3
+FEATURES = 4 * HEAD
+PAIRS = HEAD // 2
+K_PASS = 4 * P
+PASSES = DIM // K_PASS
+WORDS = DIM // 2
+TILES_PER_BATCH = SEQ // P
+GROUP = 2
+GROUPS = BATCH * TILES_PER_BATCH // GROUP
+STORE_TILES = 4
+AHEAD_T = 3
+AHEAD_Q = 2
+
+FLOPS = 2 * BATCH * SEQ * DIM * FEATURES
+
+
+def tile_attention_pa_t_kernel(tc, x, cos, sin, Wq, Wk, Wv, out_0, out_1, out_2):
+    nc = tc.nc
+    x_view = x.rearrange("b (p j) k -> b p j k", j=TILES_PER_BATCH)
+    q_view = out_0.rearrange("b h (p j) d -> b p h j d", j=TILES_PER_BATCH)
+    k_view = out_1.rearrange("b h (p j) d -> b p h j d", j=TILES_PER_BATCH)
+    v_view = out_2.rearrange("b h (p j) d -> b p h j d", j=TILES_PER_BATCH)
+
+    with ExitStack() as ctx:
+        const = ctx.enter_context(tc.tile_pool(name="const", bufs=1))
+        x_pool = ctx.enter_context(tc.tile_pool(name="x_pool", bufs=GROUPS))
+        grouped_pool = ctx.enter_context(tc.tile_pool(name="grouped_pool", bufs=3))
+        mx_pool = ctx.enter_context(tc.tile_pool(name="mx_pool", bufs=3))
+        cross_pool = ctx.enter_context(tc.tile_pool(name="cross_pool", bufs=4))
+        stage_pool = ctx.enter_context(tc.tile_pool(name="stage_pool", bufs=4))
+        psum_t = ctx.enter_context(tc.psum_pool(name="psum_t", bufs=4))
+        psum_o = ctx.enter_context(tc.psum_pool(name="psum_o", bufs=4))
+        ctx.enter_context(tc.manual_schedule())
+
+        x_tiles = {}
+        grouped_tiles = {}
+        code_tiles = {}
+        scale_tiles = {}
+        acc_tiles = {}
+        stage_tiles = {}
+
+        def place(g):
+            return divmod(g * GROUP, TILES_PER_BATCH)
+
+        def load_x(g):
+            b, j0 = place(g)
+            x_sb = x_pool.tile([P, GROUP * DIM], BF16, name="x_sb")
+            nc.sync.dma_start(
+                out=x_sb[:],
+                in_=x_view[b, :, j0 : j0 + GROUP, :].rearrange("p j k -> p (j k)"),
+            )
+            x_tiles[g] = x_sb
+
+        def load_weight(w, name):
+            cols = w.shape[1]
+            raw = const.tile([P, 2 * PASSES, 2 * cols], BF16, name=name)
+            nc.sync.dma_start(
+                out=raw[:], in_=w.rearrange("(cu p e) n -> p cu (e n)", p=P, e=2)
+            )
+            return raw
+
+        load_x(0)
+        raw_weights = [load_weight(Wq, "wq_raw"), load_weight(Wk, "wk_raw"), load_weight(Wv, "wv_raw")]
+        load_x(1)
+        cos_sb = const.tile([P, TILES_PER_BATCH, HEAD], BF16, name="cos_sb")
+        nc.sync.dma_start(out=cos_sb[:], in_=cos.rearrange("(p j) d -> p j d", j=TILES_PER_BATCH))
+        sin_sb = const.tile([P, TILES_PER_BATCH, HEAD], BF16, name="sin_sb")
+        nc.sync.dma_start(out=sin_sb[:], in_=sin.rearrange("(p j) d -> p j d", j=TILES_PER_BATCH))
+        for g in range(2, GROUPS):
+            load_x(g)
+
+        ident = const.tile([P, P], F32, name="ident")
+        make_identity(nc, ident[:])
+
+        w_grouped = const.tile([P, PASSES * FEATURES * 4], BF16, name="w_grouped", align_bytes=64)
+        w_grouped_view = w_grouped[:].rearrange("p (c n t) -> p c n t", c=PASSES, t=4)
+        first_col = 0
+        for raw in raw_weights:
+            cols = raw.shape[2] // 2
+            nc.vector.tensor_copy(
+                out=w_grouped_view[:, :, first_col : first_col + cols, :],
+                in_=raw[:].rearrange("p (c u) (e n) -> p c n (u e)", c=PASSES, e=2),
+            )
+            first_col += cols
+        w_codes = const.tile([P, PASSES * FEATURES], U32, name="w_codes", align_bytes=64)
+        w_scales = const.tile([P, PASSES * FEATURES], U8, name="w_scales", align_bytes=64)
+        nc.vector.quantize_mx(out=w_codes[:].bitcast(FP8X4), scales=w_scales[:], in_=w_grouped[:])
+
+        def transpose_group(g):
+            x_words = x_tiles[g][:].bitcast(F32)
+            grouped = grouped_pool.tile([P, GROUP * DIM], BF16, name="grouped", align_bytes=64)
+            grouped_words = grouped[:].bitcast(F32)
+            banks = []
+            for t in range(GROUP):
+                x_t = psum_t.tile([P, WORDS], F32, name="x_t")
+                for w in range(WORDS // P):
+                    first = t * WORDS + w * P
+                    nc.tensor.transpose(
+                        x_t[:, w * P : (w + 1) * P], x_words[:, first : first + P], ident[:]
+                    )
+                banks.append(x_t)
+            for t in range(GROUP):
+                nc.scalar.copy(
+                    out=grouped_words[:, t * WORDS : (t + 1) * WORDS].rearrange(
+                        "p (c r u) -> p c r u", c=PASSES, u=2
+                    ),
+                    in_=banks[t][:].rearrange("p (c u r) -> p c r u", c=PASSES, u=2),
+                )
+            grouped_tiles[g] = grouped
+
+        def quantise_group(g):
+            codes = mx_pool.tile([P, GROUP * PASSES * P], U32, name="codes", align_bytes=64)
+            scales = mx_pool.tile([P, GROUP * PASSES * P], U8, name="scales", align_bytes=64)
+            nc.vector.quantize_mx(
+                out=codes[:].bitcast(FP8X4), scales=scales[:], in_=grouped_tiles[g][:]
+            )
+            code_tiles[g] = codes
+            scale_tiles[g] = scales
+
+        def multiply_group(g):
+            acc_tiles[g] = []
+            for t in range(GROUP):
+                acc = psum_o.tile([P, FEATURES], F32, name="acc")
+                for c in range(PASSES):
+                    tokens = slice((t * PASSES + c) * P, (t * PASSES + c + 1) * P)
+                    features = slice(c * FEATURES, (c + 1) * FEATURES)
+                    nc.tensor.matmul_mx(
+                        out=acc[:],
+                        lhsT=code_tiles[g][:, tokens].bitcast(FP8X4),
+                        lhsT_scale=scale_tiles[g][:, tokens],
+                        rhs=w_codes[:, features].bitcast(FP8X4),
+                        rhs_scale=w_scales[:, features],
+                        start=(c == 0),
+                        stop=(c == PASSES - 1),
+                    )
+                acc_tiles[g].append(acc)
+
+        def rotate_group(g):
+            b, j0 = place(g)
+            for t in range(GROUP):
+                j = j0 + t
+                chunk, slot = divmod(g * GROUP + t, STORE_TILES)
+                if slot == 0:
+                    stage_tiles[chunk] = stage_pool.tile([P, 4, STORE_TILES, HEAD], F32, name="stage")
+                stage = stage_tiles[chunk]
+                acc = acc_tiles[g][t]
+                nc.scalar.copy(out=stage[:, ROTATED, slot, :], in_=acc[:, ROTATED * HEAD :])
+                heads = acc[:, : ROTATED * HEAD].rearrange("p (h d) -> p h d", h=ROTATED)
+                pairs = acc[:, : ROTATED * HEAD].rearrange("p (h i e) -> p h i e", h=ROTATED, e=2)
+                sin_pairs = sin_sb[:, j, :].rearrange("p (i e) -> p i e", e=2)
+                rotated = stage[:, :ROTATED, slot, :]
+                nc.vector.tensor_tensor(
+                    out=rotated,
+                    in0=heads,
+                    in1=cos_sb[:, j, :].unsqueeze(1).to_broadcast([P, ROTATED, HEAD]),
+                    op=MULT,
+                )
+                cross = cross_pool.tile([P, 2, ROTATED, PAIRS], F32, name="cross")
+                nc.vector.scalar_tensor_tensor(
+                    out=cross[:, 0, :, :],
+                    in0=pairs[:, :, :, 1],
+                    scalar=-1.0,
+                    in1=sin_pairs[:, :, 0].unsqueeze(1).to_broadcast([P, ROTATED, PAIRS]),
+                    op0=MULT,
+                    op1=MULT,
+                )
+                nc.vector.tensor_tensor(
+                    out=cross[:, 1, :, :],
+                    in0=pairs[:, :, :, 0],
+                    in1=sin_pairs[:, :, 1].unsqueeze(1).to_broadcast([P, ROTATED, PAIRS]),
+                    op=MULT,
+                )
+                rotated_pairs = rotated.rearrange("p h (i e) -> p h i e", e=2)
+                nc.gpsimd.tensor_tensor(
+                    out=rotated_pairs,
+                    in0=rotated_pairs,
+                    in1=cross[:].rearrange("p e h i -> p h i e"),
+                    op=ADD,
+                )
+                if slot == STORE_TILES - 1:
+                    first = j - slot
+                    rows = slice(first, first + STORE_TILES)
+                    nc.sync.dma_start(out=q_view[b, :, :, rows, :], in_=stage[:, 0:2, :, :])
+                    nc.sync.dma_start(out=k_view[b, :, 0, rows, :], in_=stage[:, 2, :, :])
+                    nc.sync.dma_start(out=v_view[b, :, 0, rows, :], in_=stage[:, 3, :, :])
+
+        for g in range(AHEAD_T):
+            transpose_group(g)
+        for g in range(AHEAD_Q):
+            quantise_group(g)
+        multiply_group(0)
+        for g in range(GROUPS):
+            if g + AHEAD_T < GROUPS:
+                transpose_group(g + AHEAD_T)
+            if g + AHEAD_Q < GROUPS:
+                quantise_group(g + AHEAD_Q)
+            if g + 1 < GROUPS:
+                multiply_group(g + 1)
+            rotate_group(g)

@@ -26,8 +26,8 @@ TILES_PER_BATCH = SEQ // P
 GROUP = 2
 GROUPS = BATCH * TILES_PER_BATCH // GROUP
 STORE_TILES = 4
-AHEAD_T = 3
-AHEAD_Q = 2
+AHEAD = 2
+TABLE_PARTS = 2
 
 FLOPS = 2 * BATCH * SEQ * DIM * FEATURES
 
@@ -77,14 +77,25 @@ def tile_attention_pa_t_kernel(tc, x, cos, sin, Wq, Wk, Wv, out_0, out_1, out_2)
             )
             return raw
 
-        load_x(0)
-        raw_weights = [load_weight(Wq, "wq_raw"), load_weight(Wk, "wk_raw"), load_weight(Wv, "wv_raw")]
-        load_x(1)
         cos_sb = const.tile([P, TILES_PER_BATCH, HEAD], BF16, name="cos_sb")
-        nc.sync.dma_start(out=cos_sb[:], in_=cos.rearrange("(p j) d -> p j d", j=TILES_PER_BATCH))
         sin_sb = const.tile([P, TILES_PER_BATCH, HEAD], BF16, name="sin_sb")
-        nc.sync.dma_start(out=sin_sb[:], in_=sin.rearrange("(p j) d -> p j d", j=TILES_PER_BATCH))
-        for g in range(2, GROUPS):
+
+        def load_tables(part):
+            tiles = slice(
+                part * TILES_PER_BATCH // TABLE_PARTS, (part + 1) * TILES_PER_BATCH // TABLE_PARTS
+            )
+            for table, table_sb in ((cos, cos_sb), (sin, sin_sb)):
+                nc.sync.dma_start(
+                    out=table_sb[:, tiles, :],
+                    in_=table.rearrange("(p j) d -> p j d", j=TILES_PER_BATCH)[:, tiles, :],
+                )
+
+        raw_weights = [load_weight(Wq, "wq_raw"), load_weight(Wk, "wk_raw"), load_weight(Wv, "wv_raw")]
+        groups_per_part = TILES_PER_BATCH // TABLE_PARTS // GROUP
+        for g in range(GROUPS):
+            part, behind = divmod(g, groups_per_part)
+            if behind == AHEAD and part < TABLE_PARTS:
+                load_tables(part)
             load_x(g)
 
         ident = const.tile([P, P], F32, name="ident")
@@ -155,27 +166,25 @@ def tile_attention_pa_t_kernel(tc, x, cos, sin, Wq, Wk, Wv, out_0, out_1, out_2)
 
         def rotate_group(g):
             b, j0 = place(g)
+            chunk, slot0 = divmod(g * GROUP, STORE_TILES)
+            if slot0 == 0:
+                stage_tiles[chunk] = stage_pool.tile([P, 4, STORE_TILES, HEAD], F32, name="stage")
+            stage = stage_tiles[chunk]
+            cross = cross_pool.tile([P, 2, ROTATED, GROUP, PAIRS], F32, name="cross")
             for t in range(GROUP):
                 j = j0 + t
-                chunk, slot = divmod(g * GROUP + t, STORE_TILES)
-                if slot == 0:
-                    stage_tiles[chunk] = stage_pool.tile([P, 4, STORE_TILES, HEAD], F32, name="stage")
-                stage = stage_tiles[chunk]
                 acc = acc_tiles[g][t]
-                nc.scalar.copy(out=stage[:, ROTATED, slot, :], in_=acc[:, ROTATED * HEAD :])
                 heads = acc[:, : ROTATED * HEAD].rearrange("p (h d) -> p h d", h=ROTATED)
                 pairs = acc[:, : ROTATED * HEAD].rearrange("p (h i e) -> p h i e", h=ROTATED, e=2)
                 sin_pairs = sin_sb[:, j, :].rearrange("p (i e) -> p i e", e=2)
-                rotated = stage[:, :ROTATED, slot, :]
                 nc.vector.tensor_tensor(
-                    out=rotated,
+                    out=stage[:, :ROTATED, slot0 + t, :],
                     in0=heads,
                     in1=cos_sb[:, j, :].unsqueeze(1).to_broadcast([P, ROTATED, HEAD]),
                     op=MULT,
                 )
-                cross = cross_pool.tile([P, 2, ROTATED, PAIRS], F32, name="cross")
                 nc.vector.scalar_tensor_tensor(
-                    out=cross[:, 0, :, :],
+                    out=cross[:, 0, :, t, :],
                     in0=pairs[:, :, :, 1],
                     scalar=-1.0,
                     in1=sin_pairs[:, :, 0].unsqueeze(1).to_broadcast([P, ROTATED, PAIRS]),
@@ -183,35 +192,37 @@ def tile_attention_pa_t_kernel(tc, x, cos, sin, Wq, Wk, Wv, out_0, out_1, out_2)
                     op1=MULT,
                 )
                 nc.vector.tensor_tensor(
-                    out=cross[:, 1, :, :],
+                    out=cross[:, 1, :, t, :],
                     in0=pairs[:, :, :, 0],
                     in1=sin_pairs[:, :, 1].unsqueeze(1).to_broadcast([P, ROTATED, PAIRS]),
                     op=MULT,
                 )
-                rotated_pairs = rotated.rearrange("p h (i e) -> p h i e", e=2)
-                nc.gpsimd.tensor_tensor(
-                    out=rotated_pairs,
-                    in0=rotated_pairs,
-                    in1=cross[:].rearrange("p e h i -> p h i e"),
-                    op=ADD,
-                )
-                if slot == STORE_TILES - 1:
-                    first = j - slot
-                    rows = slice(first, first + STORE_TILES)
-                    nc.sync.dma_start(out=q_view[b, :, :, rows, :], in_=stage[:, 0:2, :, :])
-                    nc.sync.dma_start(out=k_view[b, :, 0, rows, :], in_=stage[:, 2, :, :])
-                    nc.sync.dma_start(out=v_view[b, :, 0, rows, :], in_=stage[:, 3, :, :])
+                nc.scalar.copy(out=stage[:, ROTATED, slot0 + t, :], in_=acc[:, ROTATED * HEAD :])
+            rotated_pairs = stage[:, :ROTATED, slot0 : slot0 + GROUP, :].rearrange(
+                "p h s (i e) -> p h (s i) e", e=2
+            )
+            nc.gpsimd.tensor_tensor(
+                out=rotated_pairs,
+                in0=rotated_pairs,
+                in1=cross[:].rearrange("p e h s i -> p h (s i) e"),
+                op=ADD,
+            )
+            if slot0 + GROUP == STORE_TILES:
+                first = j0 - slot0
+                rows = slice(first, first + STORE_TILES)
+                nc.sync.dma_start(out=q_view[b, :, :, rows, :], in_=stage[:, 0:2, :, :])
+                nc.sync.dma_start(out=k_view[b, :, 0, rows, :], in_=stage[:, 2, :, :])
+                nc.sync.dma_start(out=v_view[b, :, 0, rows, :], in_=stage[:, 3, :, :])
 
-        for g in range(AHEAD_T):
+        for g in range(AHEAD):
             transpose_group(g)
-        for g in range(AHEAD_Q):
+        for g in range(AHEAD):
             quantise_group(g)
         multiply_group(0)
         for g in range(GROUPS):
-            if g + AHEAD_T < GROUPS:
-                transpose_group(g + AHEAD_T)
-            if g + AHEAD_Q < GROUPS:
-                quantise_group(g + AHEAD_Q)
+            rotate_group(g)
+            if g + AHEAD < GROUPS:
+                transpose_group(g + AHEAD)
+                quantise_group(g + AHEAD)
             if g + 1 < GROUPS:
                 multiply_group(g + 1)
-            rotate_group(g)

@@ -201,7 +201,8 @@ def tile_attention_pa_t_kernel(tc, x, cos, sin, Wq, Wk, Wv, out_0, out_1, out_2)
             rotated_pairs = stage[:, :ROTATED, slot0 : slot0 + GROUP, :].rearrange(
                 "p h s (i e) -> p h (s i) e", e=2
             )
-            nc.gpsimd.tensor_tensor(
+            adder = nc.gpsimd if g + 1 < GROUPS else nc.vector
+            adder.tensor_tensor(
                 out=rotated_pairs,
                 in0=rotated_pairs,
                 in1=cross[:].rearrange("p e h s i -> p h (s i) e"),
@@ -210,9 +211,9 @@ def tile_attention_pa_t_kernel(tc, x, cos, sin, Wq, Wk, Wv, out_0, out_1, out_2)
             if slot0 + GROUP == STORE_TILES:
                 first = j0 - slot0
                 rows = slice(first, first + STORE_TILES)
+                nc.sync.dma_start(out=v_view[b, :, 0, rows, :], in_=stage[:, 3, :, :])
                 nc.sync.dma_start(out=q_view[b, :, :, rows, :], in_=stage[:, 0:2, :, :])
                 nc.sync.dma_start(out=k_view[b, :, 0, rows, :], in_=stage[:, 2, :, :])
-                nc.sync.dma_start(out=v_view[b, :, 0, rows, :], in_=stage[:, 3, :, :])
 
         for g in range(AHEAD):
             transpose_group(g)
@@ -220,9 +221,10 @@ def tile_attention_pa_t_kernel(tc, x, cos, sin, Wq, Wk, Wv, out_0, out_1, out_2)
             quantise_group(g)
         multiply_group(0)
         for g in range(GROUPS):
-            rotate_group(g)
             if g + AHEAD < GROUPS:
                 transpose_group(g + AHEAD)
+            rotate_group(g)
+            if g + AHEAD < GROUPS:
                 quantise_group(g + AHEAD)
             if g + 1 < GROUPS:
                 multiply_group(g + 1)

@@ -164,67 +164,99 @@ def tile_attention_pa_t_kernel(tc, x, cos, sin, Wq, Wk, Wv, out_0, out_1, out_2)
                     )
                 acc_tiles[g].append(acc)
 
-        def rotate_group(g):
-            b, j0 = place(g)
-            chunk, slot0 = divmod(g * GROUP, STORE_TILES)
+        cross_tiles = {}
+
+        def slots(g):
+            return divmod(g * GROUP, STORE_TILES)
+
+        def open_group(g):
+            chunk, slot0 = slots(g)
             if slot0 == 0:
                 stage_tiles[chunk] = stage_pool.tile([P, 4, STORE_TILES, HEAD], F32, name="stage")
-            stage = stage_tiles[chunk]
-            cross = cross_pool.tile([P, 2, ROTATED, GROUP, PAIRS], F32, name="cross")
-            for t in range(GROUP):
-                j = j0 + t
-                acc = acc_tiles[g][t]
-                heads = acc[:, : ROTATED * HEAD].rearrange("p (h d) -> p h d", h=ROTATED)
-                pairs = acc[:, : ROTATED * HEAD].rearrange("p (h i e) -> p h i e", h=ROTATED, e=2)
-                sin_pairs = sin_sb[:, j, :].rearrange("p (i e) -> p i e", e=2)
-                nc.vector.tensor_tensor(
-                    out=stage[:, :ROTATED, slot0 + t, :],
-                    in0=heads,
-                    in1=cos_sb[:, j, :].unsqueeze(1).to_broadcast([P, ROTATED, HEAD]),
-                    op=MULT,
-                )
-                nc.vector.scalar_tensor_tensor(
-                    out=cross[:, 0, :, t, :],
-                    in0=pairs[:, :, :, 1],
-                    scalar=-1.0,
-                    in1=sin_pairs[:, :, 0].unsqueeze(1).to_broadcast([P, ROTATED, PAIRS]),
-                    op0=MULT,
-                    op1=MULT,
-                )
-                nc.vector.tensor_tensor(
-                    out=cross[:, 1, :, t, :],
-                    in0=pairs[:, :, :, 0],
-                    in1=sin_pairs[:, :, 1].unsqueeze(1).to_broadcast([P, ROTATED, PAIRS]),
-                    op=MULT,
-                )
-                nc.scalar.copy(out=stage[:, ROTATED, slot0 + t, :], in_=acc[:, ROTATED * HEAD :])
-            rotated_pairs = stage[:, :ROTATED, slot0 : slot0 + GROUP, :].rearrange(
+            cross_tiles[g] = cross_pool.tile([P, 2, ROTATED, GROUP, PAIRS], F32, name="cross")
+
+        def cos_product(g, t):
+            chunk, slot0 = slots(g)
+            j = place(g)[1] + t
+            nc.vector.tensor_tensor(
+                out=stage_tiles[chunk][:, :ROTATED, slot0 + t, :],
+                in0=acc_tiles[g][t][:, : ROTATED * HEAD].rearrange("p (h d) -> p h d", h=ROTATED),
+                in1=cos_sb[:, j, :].unsqueeze(1).to_broadcast([P, ROTATED, HEAD]),
+                op=MULT,
+            )
+
+        def sin_product(g, t, plane):
+            j = place(g)[1] + t
+            pairs = acc_tiles[g][t][:, : ROTATED * HEAD].rearrange(
+                "p (h i e) -> p h i e", h=ROTATED, e=2
+            )
+            sin_pairs = sin_sb[:, j, :].rearrange("p (i e) -> p i e", e=2)
+            nc.vector.scalar_tensor_tensor(
+                out=cross_tiles[g][:, plane, :, t, :],
+                in0=pairs[:, :, :, 1 - plane],
+                scalar=(-1.0, 1.0)[plane],
+                in1=sin_pairs[:, :, plane].unsqueeze(1).to_broadcast([P, ROTATED, PAIRS]),
+                op0=MULT,
+                op1=MULT,
+            )
+
+        def copy_v(g, t):
+            chunk, slot0 = slots(g)
+            nc.scalar.copy(
+                out=stage_tiles[chunk][:, ROTATED, slot0 + t, :],
+                in_=acc_tiles[g][t][:, ROTATED * HEAD :],
+            )
+
+        def add_partner(engine, g, heads):
+            chunk, slot0 = slots(g)
+            rotated_pairs = stage_tiles[chunk][:, heads, slot0 : slot0 + GROUP, :].rearrange(
                 "p h s (i e) -> p h (s i) e", e=2
             )
-            adder = nc.gpsimd if g + 1 < GROUPS else nc.vector
-            adder.tensor_tensor(
+            engine.tensor_tensor(
                 out=rotated_pairs,
                 in0=rotated_pairs,
-                in1=cross[:].rearrange("p e h s i -> p h (s i) e"),
+                in1=cross_tiles[g][:, :, heads, :, :].rearrange("p e h s i -> p h (s i) e"),
                 op=ADD,
             )
-            if slot0 + GROUP == STORE_TILES:
-                first = j0 - slot0
-                rows = slice(first, first + STORE_TILES)
-                nc.sync.dma_start(out=v_view[b, :, 0, rows, :], in_=stage[:, 3, :, :])
-                nc.sync.dma_start(out=q_view[b, :, :, rows, :], in_=stage[:, 0:2, :, :])
-                nc.sync.dma_start(out=k_view[b, :, 0, rows, :], in_=stage[:, 2, :, :])
+
+        def store_chunk(chunk):
+            b, first = divmod(chunk * STORE_TILES, TILES_PER_BATCH)
+            rows = slice(first, first + STORE_TILES)
+            stage = stage_tiles[chunk]
+            nc.sync.dma_start(out=v_view[b, :, 0, rows, :], in_=stage[:, 3, :, :])
+            nc.sync.dma_start(out=q_view[b, :, :, rows, :], in_=stage[:, 0:2, :, :])
+            nc.sync.dma_start(out=k_view[b, :, 0, rows, :], in_=stage[:, 2, :, :])
+
+        Q_HEADS = slice(0, 2)
+        K_HEAD = slice(2, 3)
+        LAST = GROUP - 1
 
         for g in range(AHEAD):
             transpose_group(g)
         for g in range(AHEAD):
             quantise_group(g)
         multiply_group(0)
-        for g in range(GROUPS):
+        for g in range(GROUPS + 1):
+            if g < GROUPS:
+                open_group(g)
+                for t in range(GROUP):
+                    copy_v(g, t)
             if g + AHEAD < GROUPS:
                 transpose_group(g + AHEAD)
-            rotate_group(g)
+            if g < GROUPS:
+                for t in range(GROUP):
+                    cos_product(g, t)
+                    sin_product(g, t, 0)
+                    if t < LAST:
+                        sin_product(g, t, 1)
             if g + AHEAD < GROUPS:
                 quantise_group(g + AHEAD)
+            if g >= 1:
+                add_partner(nc.vector, g - 1, K_HEAD)
+                if slots(g)[1] == 0:
+                    store_chunk(slots(g - 1)[0])
+            if g < GROUPS:
+                sin_product(g, LAST, 1)
+                add_partner(nc.gpsimd if g + 1 < GROUPS else nc.vector, g, Q_HEADS)
             if g + 1 < GROUPS:
                 multiply_group(g + 1)

@@ -25,9 +25,13 @@ WORDS = DIM // 2
 TILES_PER_BATCH = SEQ // P
 GROUP = 2
 GROUPS = BATCH * TILES_PER_BATCH // GROUP
-STORE_TILES = 4
+ROUND = 4
+ROUNDS = BATCH * TILES_PER_BATCH // ROUND
+GROUPS_PER_ROUND = ROUND // GROUP
 AHEAD = 2
 TABLE_PARTS = 2
+T_BANKS = 3
+ACC_BANKS = 5
 
 FLOPS = 2 * BATCH * SEQ * DIM * FEATURES
 
@@ -42,12 +46,12 @@ def tile_attention_pa_t_kernel(tc, x, cos, sin, Wq, Wk, Wv, out_0, out_1, out_2)
     with ExitStack() as ctx:
         const = ctx.enter_context(tc.tile_pool(name="const", bufs=1))
         x_pool = ctx.enter_context(tc.tile_pool(name="x_pool", bufs=GROUPS))
-        grouped_pool = ctx.enter_context(tc.tile_pool(name="grouped_pool", bufs=3))
-        mx_pool = ctx.enter_context(tc.tile_pool(name="mx_pool", bufs=3))
-        cross_pool = ctx.enter_context(tc.tile_pool(name="cross_pool", bufs=4))
-        stage_pool = ctx.enter_context(tc.tile_pool(name="stage_pool", bufs=4))
-        psum_t = ctx.enter_context(tc.psum_pool(name="psum_t", bufs=4))
-        psum_o = ctx.enter_context(tc.psum_pool(name="psum_o", bufs=4))
+        grouped_pool = ctx.enter_context(tc.tile_pool(name="grouped_pool", bufs=4))
+        mx_pool = ctx.enter_context(tc.tile_pool(name="mx_pool", bufs=3 * GROUPS_PER_ROUND))
+        cross_pool = ctx.enter_context(tc.tile_pool(name="cross_pool", bufs=3))
+        stage_pool = ctx.enter_context(tc.tile_pool(name="stage_pool", bufs=3))
+        psum_t = ctx.enter_context(tc.psum_pool(name="psum_t", bufs=T_BANKS))
+        psum_o = ctx.enter_context(tc.psum_pool(name="psum_o", bufs=ACC_BANKS))
         ctx.enter_context(tc.manual_schedule())
 
         x_tiles = {}
@@ -56,6 +60,7 @@ def tile_attention_pa_t_kernel(tc, x, cos, sin, Wq, Wk, Wv, out_0, out_1, out_2)
         scale_tiles = {}
         acc_tiles = {}
         stage_tiles = {}
+        cross_tiles = {}
 
         def place(g):
             return divmod(g * GROUP, TILES_PER_BATCH)
@@ -90,12 +95,16 @@ def tile_attention_pa_t_kernel(tc, x, cos, sin, Wq, Wk, Wv, out_0, out_1, out_2)
                     in_=table.rearrange("(p j) d -> p j d", j=TILES_PER_BATCH)[:, tiles, :],
                 )
 
-        raw_weights = [load_weight(Wq, "wq_raw"), load_weight(Wk, "wk_raw"), load_weight(Wv, "wv_raw")]
-        groups_per_part = TILES_PER_BATCH // TABLE_PARTS // GROUP
-        for g in range(GROUPS):
-            part, behind = divmod(g, groups_per_part)
-            if behind == AHEAD and part < TABLE_PARTS:
-                load_tables(part)
+        wq_raw = load_weight(Wq, "wq_raw")
+        wk_raw = load_weight(Wk, "wk_raw")
+        wv_raw = load_weight(Wv, "wv_raw")
+        load_x(0)
+        load_x(1)
+        load_tables(0)
+        for g in range(2, 6):
+            load_x(g)
+        load_tables(1)
+        for g in range(6, GROUPS):
             load_x(g)
 
         ident = const.tile([P, P], F32, name="ident")
@@ -104,7 +113,7 @@ def tile_attention_pa_t_kernel(tc, x, cos, sin, Wq, Wk, Wv, out_0, out_1, out_2)
         w_grouped = const.tile([P, PASSES * FEATURES * 4], BF16, name="w_grouped", align_bytes=64)
         w_grouped_view = w_grouped[:].rearrange("p (c n t) -> p c n t", c=PASSES, t=4)
         first_col = 0
-        for raw in raw_weights:
+        for raw in (wq_raw, wk_raw, wv_raw):
             cols = raw.shape[2] // 2
             nc.vector.tensor_copy(
                 out=w_grouped_view[:, :, first_col : first_col + cols, :],
@@ -119,7 +128,6 @@ def tile_attention_pa_t_kernel(tc, x, cos, sin, Wq, Wk, Wv, out_0, out_1, out_2)
             x_words = x_tiles[g][:].bitcast(F32)
             grouped = grouped_pool.tile([P, GROUP * DIM], BF16, name="grouped", align_bytes=64)
             grouped_words = grouped[:].bitcast(F32)
-            banks = []
             for t in range(GROUP):
                 x_t = psum_t.tile([P, WORDS], F32, name="x_t")
                 for w in range(WORDS // P):
@@ -127,13 +135,11 @@ def tile_attention_pa_t_kernel(tc, x, cos, sin, Wq, Wk, Wv, out_0, out_1, out_2)
                     nc.tensor.transpose(
                         x_t[:, w * P : (w + 1) * P], x_words[:, first : first + P], ident[:]
                     )
-                banks.append(x_t)
-            for t in range(GROUP):
                 nc.scalar.copy(
                     out=grouped_words[:, t * WORDS : (t + 1) * WORDS].rearrange(
                         "p (c r u) -> p c r u", c=PASSES, u=2
                     ),
-                    in_=banks[t][:].rearrange("p (c u r) -> p c r u", c=PASSES, u=2),
+                    in_=x_t[:].rearrange("p (c u r) -> p c r u", c=PASSES, u=2),
                 )
             grouped_tiles[g] = grouped
 
@@ -147,7 +153,6 @@ def tile_attention_pa_t_kernel(tc, x, cos, sin, Wq, Wk, Wv, out_0, out_1, out_2)
             scale_tiles[g] = scales
 
         def multiply_group(g):
-            acc_tiles[g] = []
             for t in range(GROUP):
                 acc = psum_o.tile([P, FEATURES], F32, name="acc")
                 for c in range(PASSES):
@@ -162,37 +167,37 @@ def tile_attention_pa_t_kernel(tc, x, cos, sin, Wq, Wk, Wv, out_0, out_1, out_2)
                         start=(c == 0),
                         stop=(c == PASSES - 1),
                     )
-                acc_tiles[g].append(acc)
+                acc_tiles[g * GROUP + t] = acc
 
-        cross_tiles = {}
+        def open_round(r):
+            stage_tiles[r] = stage_pool.tile([P, 4, ROUND, HEAD], F32, name="stage")
+            cross_tiles[r] = cross_pool.tile([P, 2, ROTATED, ROUND, PAIRS], F32, name="cross")
 
-        def slots(g):
-            return divmod(g * GROUP, STORE_TILES)
+        def copy_v(r, t):
+            nc.scalar.copy(
+                out=stage_tiles[r][:, ROTATED, t, :],
+                in_=acc_tiles[r * ROUND + t][:, ROTATED * HEAD :],
+            )
 
-        def open_group(g):
-            chunk, slot0 = slots(g)
-            if slot0 == 0:
-                stage_tiles[chunk] = stage_pool.tile([P, 4, STORE_TILES, HEAD], F32, name="stage")
-            cross_tiles[g] = cross_pool.tile([P, 2, ROTATED, GROUP, PAIRS], F32, name="cross")
-
-        def cos_product(g, t):
-            chunk, slot0 = slots(g)
-            j = place(g)[1] + t
+        def cos_product(r, t):
+            j = (r * ROUND + t) % TILES_PER_BATCH
             nc.vector.tensor_tensor(
-                out=stage_tiles[chunk][:, :ROTATED, slot0 + t, :],
-                in0=acc_tiles[g][t][:, : ROTATED * HEAD].rearrange("p (h d) -> p h d", h=ROTATED),
+                out=stage_tiles[r][:, :ROTATED, t, :],
+                in0=acc_tiles[r * ROUND + t][:, : ROTATED * HEAD].rearrange(
+                    "p (h d) -> p h d", h=ROTATED
+                ),
                 in1=cos_sb[:, j, :].unsqueeze(1).to_broadcast([P, ROTATED, HEAD]),
                 op=MULT,
             )
 
-        def sin_product(g, t, plane):
-            j = place(g)[1] + t
-            pairs = acc_tiles[g][t][:, : ROTATED * HEAD].rearrange(
+        def sin_product(r, t, plane):
+            j = (r * ROUND + t) % TILES_PER_BATCH
+            pairs = acc_tiles[r * ROUND + t][:, : ROTATED * HEAD].rearrange(
                 "p (h i e) -> p h i e", h=ROTATED, e=2
             )
             sin_pairs = sin_sb[:, j, :].rearrange("p (i e) -> p i e", e=2)
             nc.vector.scalar_tensor_tensor(
-                out=cross_tiles[g][:, plane, :, t, :],
+                out=cross_tiles[r][:, plane, :, t, :],
                 in0=pairs[:, :, :, 1 - plane],
                 scalar=(-1.0, 1.0)[plane],
                 in1=sin_pairs[:, :, plane].unsqueeze(1).to_broadcast([P, ROTATED, PAIRS]),
@@ -200,63 +205,51 @@ def tile_attention_pa_t_kernel(tc, x, cos, sin, Wq, Wk, Wv, out_0, out_1, out_2)
                 op1=MULT,
             )
 
-        def copy_v(g, t):
-            chunk, slot0 = slots(g)
-            nc.scalar.copy(
-                out=stage_tiles[chunk][:, ROTATED, slot0 + t, :],
-                in_=acc_tiles[g][t][:, ROTATED * HEAD :],
-            )
-
-        def add_partner(engine, g, heads):
-            chunk, slot0 = slots(g)
-            rotated_pairs = stage_tiles[chunk][:, heads, slot0 : slot0 + GROUP, :].rearrange(
+        def add_partner(engine, r):
+            rotated_pairs = stage_tiles[r][:, :ROTATED, :, :].rearrange(
                 "p h s (i e) -> p h (s i) e", e=2
             )
             engine.tensor_tensor(
                 out=rotated_pairs,
                 in0=rotated_pairs,
-                in1=cross_tiles[g][:, :, heads, :, :].rearrange("p e h s i -> p h (s i) e"),
+                in1=cross_tiles[r][:].rearrange("p e h s i -> p h (s i) e"),
                 op=ADD,
             )
 
-        def store_chunk(chunk):
-            b, first = divmod(chunk * STORE_TILES, TILES_PER_BATCH)
-            rows = slice(first, first + STORE_TILES)
-            stage = stage_tiles[chunk]
+        def store_round(r):
+            b, j0 = divmod(r * ROUND, TILES_PER_BATCH)
+            rows = slice(j0, j0 + ROUND)
+            stage = stage_tiles[r]
             nc.sync.dma_start(out=v_view[b, :, 0, rows, :], in_=stage[:, 3, :, :])
             nc.sync.dma_start(out=q_view[b, :, :, rows, :], in_=stage[:, 0:2, :, :])
             nc.sync.dma_start(out=k_view[b, :, 0, rows, :], in_=stage[:, 2, :, :])
 
-        Q_HEADS = slice(0, 2)
-        K_HEAD = slice(2, 3)
-        LAST = GROUP - 1
-
-        for g in range(AHEAD):
+        LAST = ROUND - 1
+        for g in range(GROUPS_PER_ROUND):
             transpose_group(g)
-        for g in range(AHEAD):
+        for g in range(GROUPS_PER_ROUND):
             quantise_group(g)
-        multiply_group(0)
-        for g in range(GROUPS + 1):
-            if g < GROUPS:
-                open_group(g)
-                for t in range(GROUP):
-                    copy_v(g, t)
-            if g + AHEAD < GROUPS:
-                transpose_group(g + AHEAD)
-            if g < GROUPS:
-                for t in range(GROUP):
-                    cos_product(g, t)
-                    sin_product(g, t, 0)
-                    if t < LAST:
-                        sin_product(g, t, 1)
-            if g + AHEAD < GROUPS:
-                quantise_group(g + AHEAD)
-            if g >= 1:
-                add_partner(nc.vector, g - 1, K_HEAD)
-                if slots(g)[1] == 0:
-                    store_chunk(slots(g - 1)[0])
-            if g < GROUPS:
-                sin_product(g, LAST, 1)
-                add_partner(nc.gpsimd if g + 1 < GROUPS else nc.vector, g, Q_HEADS)
-            if g + 1 < GROUPS:
-                multiply_group(g + 1)
+            multiply_group(g)
+        prepared = GROUPS_PER_ROUND
+        for r in range(ROUNDS):
+            wanted = min(GROUPS, (r + 1 + AHEAD) * GROUPS_PER_ROUND)
+            due = range(prepared, wanted)
+            prepared = wanted
+            open_round(r)
+            for t in range(ROUND):
+                copy_v(r, t)
+            for g in due:
+                transpose_group(g)
+            for t in range(ROUND):
+                cos_product(r, t)
+                sin_product(r, t, 0)
+                if t < LAST:
+                    sin_product(r, t, 1)
+            for g in due:
+                quantise_group(g)
+            sin_product(r, LAST, 1)
+            add_partner(nc.gpsimd if r + 1 < ROUNDS else nc.vector, r)
+            store_round(r)
+            if r + 1 < ROUNDS:
+                for g in range((r + 1) * GROUPS_PER_ROUND, (r + 2) * GROUPS_PER_ROUND):
+                    multiply_group(g)

@@ -30,6 +30,7 @@ ROUNDS = BATCH * TILES_PER_BATCH // ROUND
 GROUPS_PER_ROUND = ROUND // GROUP
 AHEAD = 2
 TABLE_PARTS = 2
+VECTOR_ADDS = 1
 T_BANKS = 3
 ACC_BANKS = 5
 
@@ -96,15 +97,16 @@ def tile_attention_pa_t_kernel(tc, x, cos, sin, Wq, Wk, Wv, out_0, out_1, out_2)
                 )
 
         wq_raw = load_weight(Wq, "wq_raw")
+        load_x(0)
         wk_raw = load_weight(Wk, "wk_raw")
         wv_raw = load_weight(Wv, "wv_raw")
-        load_x(0)
         load_x(1)
         load_tables(0)
-        for g in range(2, 6):
+        first_rounds = (1 + AHEAD) * GROUPS_PER_ROUND
+        for g in range(GROUPS_PER_ROUND, first_rounds):
             load_x(g)
         load_tables(1)
-        for g in range(6, GROUPS):
+        for g in range(first_rounds, GROUPS):
             load_x(g)
 
         ident = const.tile([P, P], F32, name="ident")
@@ -205,14 +207,14 @@ def tile_attention_pa_t_kernel(tc, x, cos, sin, Wq, Wk, Wv, out_0, out_1, out_2)
                 op1=MULT,
             )
 
-        def add_partner(engine, r):
-            rotated_pairs = stage_tiles[r][:, :ROTATED, :, :].rearrange(
+        def add_partner(engine, r, tiles):
+            rotated_pairs = stage_tiles[r][:, :ROTATED, tiles, :].rearrange(
                 "p h s (i e) -> p h (s i) e", e=2
             )
             engine.tensor_tensor(
                 out=rotated_pairs,
                 in0=rotated_pairs,
-                in1=cross_tiles[r][:].rearrange("p e h s i -> p h (s i) e"),
+                in1=cross_tiles[r][:, :, :, tiles, :].rearrange("p e h s i -> p h (s i) e"),
                 op=ADD,
             )
 
@@ -247,8 +249,9 @@ def tile_attention_pa_t_kernel(tc, x, cos, sin, Wq, Wk, Wv, out_0, out_1, out_2)
                     sin_product(r, t, 1)
             for g in due:
                 quantise_group(g)
+            add_partner(nc.vector, r, slice(0, VECTOR_ADDS))
             sin_product(r, LAST, 1)
-            add_partner(nc.gpsimd if r + 1 < ROUNDS else nc.vector, r)
+            add_partner(nc.gpsimd if r + 1 < ROUNDS else nc.vector, r, slice(VECTOR_ADDS, ROUND))
             store_round(r)
             if r + 1 < ROUNDS:
                 for g in range((r + 1) * GROUPS_PER_ROUND, (r + 2) * GROUPS_PER_ROUND):

@@ -10,6 +10,7 @@ U8 = mybir.dt.uint8
 FP8X4 = mybir.dt.float8_e4m3fn_x4
 MULT = mybir.AluOpType.mult
 ADD = mybir.AluOpType.add
+COPY = mybir.ActivationFunctionType.Copy
 
 P = 128
 BATCH = 2
@@ -96,6 +97,13 @@ def tile_attention_pa_t_kernel(tc, x, cos, sin, Wq, Wk, Wv, out_0, out_1, out_2)
                     in_=table.rearrange("(p j) d -> p j d", j=TILES_PER_BATCH)[:, tiles, :],
                 )
 
+        def sign_table(part):
+            tiles = slice(
+                part * TILES_PER_BATCH // TABLE_PARTS, (part + 1) * TILES_PER_BATCH // TABLE_PARTS
+            )
+            even = sin_sb[:, tiles, :].rearrange("p j (i e) -> p j i e", e=2)[:, :, :, 0]
+            nc.scalar.activation(out=even, in_=even, func=COPY, scale=-1.0)
+
         wq_raw = load_weight(Wq, "wq_raw")
         load_x(0)
         wk_raw = load_weight(Wk, "wk_raw")
@@ -173,7 +181,7 @@ def tile_attention_pa_t_kernel(tc, x, cos, sin, Wq, Wk, Wv, out_0, out_1, out_2)
 
         def open_round(r):
             stage_tiles[r] = stage_pool.tile([P, 4, ROUND, HEAD], F32, name="stage")
-            cross_tiles[r] = cross_pool.tile([P, 2, ROTATED, ROUND, PAIRS], F32, name="cross")
+            cross_tiles[r] = cross_pool.tile([P, ROTATED, ROUND, HEAD], F32, name="cross")
 
         def copy_v(r, t):
             nc.scalar.copy(
@@ -192,30 +200,25 @@ def tile_attention_pa_t_kernel(tc, x, cos, sin, Wq, Wk, Wv, out_0, out_1, out_2)
                 op=MULT,
             )
 
-        def sin_product(r, t, plane):
+        def sin_product(r, t):
             j = (r * ROUND + t) % TILES_PER_BATCH
             pairs = acc_tiles[r * ROUND + t][:, : ROTATED * HEAD].rearrange(
                 "p (h i e) -> p h i e", h=ROTATED, e=2
             )
-            sin_pairs = sin_sb[:, j, :].rearrange("p (i e) -> p i e", e=2)
-            nc.vector.scalar_tensor_tensor(
-                out=cross_tiles[r][:, plane, :, t, :],
-                in0=pairs[:, :, :, 1 - plane],
-                scalar=(-1.0, 1.0)[plane],
-                in1=sin_pairs[:, :, plane].unsqueeze(1).to_broadcast([P, ROTATED, PAIRS]),
-                op0=MULT,
-                op1=MULT,
+            nc.vector.tensor_tensor(
+                out=cross_tiles[r][:, :, t, :].rearrange("p h (i e) -> p h i e", e=2),
+                in0=pairs[:, :, :, ::-1],
+                in1=sin_sb[:, j, :]
+                .rearrange("p (i e) -> p i e", e=2)
+                .unsqueeze(1)
+                .to_broadcast([P, ROTATED, PAIRS, 2]),
+                op=MULT,
             )
 
         def add_partner(engine, r, tiles):
-            rotated_pairs = stage_tiles[r][:, :ROTATED, tiles, :].rearrange(
-                "p h s (i e) -> p h (s i) e", e=2
-            )
+            rotated = stage_tiles[r][:, :ROTATED, tiles, :]
             engine.tensor_tensor(
-                out=rotated_pairs,
-                in0=rotated_pairs,
-                in1=cross_tiles[r][:, :, :, tiles, :].rearrange("p e h s i -> p h (s i) e"),
-                op=ADD,
+                out=rotated, in0=rotated, in1=cross_tiles[r][:, :, tiles, :], op=ADD
             )
 
         def store_round(r):
@@ -229,6 +232,8 @@ def tile_attention_pa_t_kernel(tc, x, cos, sin, Wq, Wk, Wv, out_0, out_1, out_2)
         LAST = ROUND - 1
         for g in range(GROUPS_PER_ROUND):
             transpose_group(g)
+        for part in range(TABLE_PARTS):
+            sign_table(part)
         for g in range(GROUPS_PER_ROUND):
             quantise_group(g)
             multiply_group(g)
@@ -244,13 +249,12 @@ def tile_attention_pa_t_kernel(tc, x, cos, sin, Wq, Wk, Wv, out_0, out_1, out_2)
                 transpose_group(g)
             for t in range(ROUND):
                 cos_product(r, t)
-                sin_product(r, t, 0)
                 if t < LAST:
-                    sin_product(r, t, 1)
+                    sin_product(r, t)
             for g in due:
                 quantise_group(g)
             add_partner(nc.vector, r, slice(0, VECTOR_ADDS))
-            sin_product(r, LAST, 1)
+            sin_product(r, LAST)
             add_partner(nc.gpsimd if r + 1 < ROUNDS else nc.vector, r, slice(VECTOR_ADDS, ROUND))
             store_round(r)
             if r + 1 < ROUNDS:

@@ -232,8 +232,7 @@ def tile_attention_pa_t_kernel(tc, x, cos, sin, Wq, Wk, Wv, out_0, out_1, out_2)
         LAST = ROUND - 1
         for g in range(GROUPS_PER_ROUND):
             transpose_group(g)
-        for part in range(TABLE_PARTS):
-            sign_table(part)
+        sign_table(0)
         for g in range(GROUPS_PER_ROUND):
             quantise_group(g)
             multiply_group(g)
@@ -247,6 +246,8 @@ def tile_attention_pa_t_kernel(tc, x, cos, sin, Wq, Wk, Wv, out_0, out_1, out_2)
                 copy_v(r, t)
             for g in due:
                 transpose_group(g)
+            if 0 < r < TABLE_PARTS:
+                sign_table(r)
             for t in range(ROUND):
                 cos_product(r, t)
                 if t < LAST:

@@ -29,6 +29,8 @@ GROUPS = BATCH * TILES_PER_BATCH // GROUP
 ROUND = 4
 ROUNDS = BATCH * TILES_PER_BATCH // ROUND
 GROUPS_PER_ROUND = ROUND // GROUP
+LOAD = 4
+STORE = 8
 AHEAD = 2
 TABLE_PARTS = 2
 VECTOR_ADDS = 1
@@ -47,11 +49,11 @@ def tile_attention_pa_t_kernel(tc, x, cos, sin, Wq, Wk, Wv, out_0, out_1, out_2)
 
     with ExitStack() as ctx:
         const = ctx.enter_context(tc.tile_pool(name="const", bufs=1))
-        x_pool = ctx.enter_context(tc.tile_pool(name="x_pool", bufs=GROUPS))
+        x_pool = ctx.enter_context(tc.tile_pool(name="x_pool", bufs=BATCH * TILES_PER_BATCH // LOAD))
         grouped_pool = ctx.enter_context(tc.tile_pool(name="grouped_pool", bufs=4))
         mx_pool = ctx.enter_context(tc.tile_pool(name="mx_pool", bufs=3 * GROUPS_PER_ROUND))
         cross_pool = ctx.enter_context(tc.tile_pool(name="cross_pool", bufs=3))
-        stage_pool = ctx.enter_context(tc.tile_pool(name="stage_pool", bufs=3))
+        stage_pool = ctx.enter_context(tc.tile_pool(name="stage_pool", bufs=4))
         psum_t = ctx.enter_context(tc.psum_pool(name="psum_t", bufs=T_BANKS))
         psum_o = ctx.enter_context(tc.psum_pool(name="psum_o", bufs=ACC_BANKS))
         ctx.enter_context(tc.manual_schedule())
@@ -62,19 +64,18 @@ def tile_attention_pa_t_kernel(tc, x, cos, sin, Wq, Wk, Wv, out_0, out_1, out_2)
         scale_tiles = {}
         acc_tiles = {}
         stage_tiles = {}
+        store_tiles = {}
         cross_tiles = {}
 
-        def place(g):
-            return divmod(g * GROUP, TILES_PER_BATCH)
-
-        def load_x(g):
-            b, j0 = place(g)
-            x_sb = x_pool.tile([P, GROUP * DIM], BF16, name="x_sb")
+        def load_x(first, count):
+            q, t = divmod(first, LOAD)
+            b, j0 = divmod(first, TILES_PER_BATCH)
+            if t == 0:
+                x_tiles[q] = x_pool.tile([P, LOAD * DIM], BF16, name="x_sb")
             nc.sync.dma_start(
-                out=x_sb[:],
-                in_=x_view[b, :, j0 : j0 + GROUP, :].rearrange("p j k -> p (j k)"),
+                out=x_tiles[q][:, t * DIM : (t + count) * DIM],
+                in_=x_view[b, :, j0 : j0 + count, :].rearrange("p j k -> p (j k)"),
             )
-            x_tiles[g] = x_sb
 
         def load_weight(w, name):
             cols = w.shape[1]
@@ -105,17 +106,16 @@ def tile_attention_pa_t_kernel(tc, x, cos, sin, Wq, Wk, Wv, out_0, out_1, out_2)
             nc.scalar.activation(out=even, in_=even, func=COPY, scale=-1.0)
 
         wq_raw = load_weight(Wq, "wq_raw")
-        load_x(0)
+        load_x(0, GROUP)
         wk_raw = load_weight(Wk, "wk_raw")
         wv_raw = load_weight(Wv, "wv_raw")
-        load_x(1)
+        load_x(GROUP, GROUP)
         load_tables(0)
-        first_rounds = (1 + AHEAD) * GROUPS_PER_ROUND
-        for g in range(GROUPS_PER_ROUND, first_rounds):
-            load_x(g)
+        for first in range(LOAD, 3 * LOAD, LOAD):
+            load_x(first, LOAD)
         load_tables(1)
-        for g in range(first_rounds, GROUPS):
-            load_x(g)
+        for first in range(3 * LOAD, BATCH * TILES_PER_BATCH, LOAD):
+            load_x(first, LOAD)
 
         ident = const.tile([P, P], F32, name="ident")
         make_identity(nc, ident[:])
@@ -135,7 +135,8 @@ def tile_attention_pa_t_kernel(tc, x, cos, sin, Wq, Wk, Wv, out_0, out_1, out_2)
         nc.vector.quantize_mx(out=w_codes[:].bitcast(FP8X4), scales=w_scales[:], in_=w_grouped[:])
 
         def transpose_group(g):
-            x_words = x_tiles[g][:].bitcast(F32)
+            q, half = divmod(g * GROUP, LOAD)
+            x_words = x_tiles[q][:, half * DIM : (half + GROUP) * DIM].bitcast(F32)
             grouped = grouped_pool.tile([P, GROUP * DIM], BF16, name="grouped", align_bytes=64)
             grouped_words = grouped[:].bitcast(F32)
             for t in range(GROUP):
@@ -180,7 +181,11 @@ def tile_attention_pa_t_kernel(tc, x, cos, sin, Wq, Wk, Wv, out_0, out_1, out_2)
                 acc_tiles[g * GROUP + t] = acc
 
         def open_round(r):
-            stage_tiles[r] = stage_pool.tile([P, 4, ROUND, HEAD], F32, name="stage")
+            if r * ROUND % STORE == 0:
+                stage = stage_pool.tile([P, 4, STORE, HEAD], F32, name="stage")
+                for i in range(STORE // ROUND):
+                    stage_tiles[r + i] = stage[:, :, i * ROUND : (i + 1) * ROUND, :]
+                store_tiles[r * ROUND // STORE] = stage
             cross_tiles[r] = cross_pool.tile([P, ROTATED, ROUND, HEAD], F32, name="cross")
 
         def copy_v(r, t):
@@ -221,10 +226,11 @@ def tile_attention_pa_t_kernel(tc, x, cos, sin, Wq, Wk, Wv, out_0, out_1, out_2)
                 out=rotated, in0=rotated, in1=cross_tiles[r][:, :, tiles, :], op=ADD
             )
 
-        def store_round(r):
-            b, j0 = divmod(r * ROUND, TILES_PER_BATCH)
-            rows = slice(j0, j0 + ROUND)
-            stage = stage_tiles[r]
+        def store_tiles_of(first, count):
+            b, j0 = divmod(first, TILES_PER_BATCH)
+            rows = slice(j0, j0 + count)
+            s, t = divmod(first, STORE)
+            stage = store_tiles[s][:, :, t : t + count, :]
             nc.sync.dma_start(out=v_view[b, :, 0, rows, :], in_=stage[:, 3, :, :])
             nc.sync.dma_start(out=q_view[b, :, :, rows, :], in_=stage[:, 0:2, :, :])
             nc.sync.dma_start(out=k_view[b, :, 0, rows, :], in_=stage[:, 2, :, :])
@@ -257,7 +263,10 @@ def tile_attention_pa_t_kernel(tc, x, cos, sin, Wq, Wk, Wv, out_0, out_1, out_2)
             add_partner(nc.vector, r, slice(0, VECTOR_ADDS))
             sin_product(r, LAST)
             add_partner(nc.gpsimd if r + 1 < ROUNDS else nc.vector, r, slice(VECTOR_ADDS, ROUND))
-            store_round(r)
+            if r + 2 >= ROUNDS:
+                store_tiles_of(r * ROUND, ROUND)
+            elif (r + 1) * ROUND % STORE == 0:
+                store_tiles_of((r + 1) * ROUND - STORE, STORE)
             if r + 1 < ROUNDS:
                 for g in range((r + 1) * GROUPS_PER_ROUND, (r + 2) * GROUPS_PER_ROUND):
                     multiply_group(g)

@@ -105,9 +105,16 @@ def tile_attention_pa_t_kernel(tc, x, cos, sin, Wq, Wk, Wv, out_0, out_1, out_2)
             even = sin_sb[:, tiles, :].rearrange("p j (i e) -> p j i e", e=2)[:, :, :, 0]
             nc.scalar.activation(out=even, in_=even, func=COPY, scale=-1.0)
 
-        wq_raw = load_weight(Wq, "wq_raw")
-        load_x(0, GROUP)
+        load_x(0, 1)
+        wq_raw = const.tile([P, 2 * PASSES, 2 * Wq.shape[1]], BF16, name="wq_raw")
+        for c in range(PASSES):
+            halves = slice(2 * c, 2 * c + 2)
+            nc.sync.dma_start(
+                out=wq_raw[:, halves, :],
+                in_=Wq.rearrange("(cu p e) n -> p cu (e n)", p=P, e=2)[:, halves, :],
+            )
         wk_raw = load_weight(Wk, "wk_raw")
+        load_x(1, 1)
         wv_raw = load_weight(Wv, "wv_raw")
         load_x(GROUP, GROUP)
         load_tables(0)
@@ -122,49 +129,77 @@ def tile_attention_pa_t_kernel(tc, x, cos, sin, Wq, Wk, Wv, out_0, out_1, out_2)
 
         w_grouped = const.tile([P, PASSES * FEATURES * 4], BF16, name="w_grouped", align_bytes=64)
         w_grouped_view = w_grouped[:].rearrange("p (c n t) -> p c n t", c=PASSES, t=4)
-        first_col = 0
-        for raw in (wq_raw, wk_raw, wv_raw):
-            cols = raw.shape[2] // 2
-            nc.vector.tensor_copy(
-                out=w_grouped_view[:, :, first_col : first_col + cols, :],
-                in_=raw[:].rearrange("p (c u) (e n) -> p c n (u e)", c=PASSES, e=2),
-            )
-            first_col += cols
         w_codes = const.tile([P, PASSES * FEATURES], U32, name="w_codes", align_bytes=64)
         w_scales = const.tile([P, PASSES * FEATURES], U8, name="w_scales", align_bytes=64)
-        nc.vector.quantize_mx(out=w_codes[:].bitcast(FP8X4), scales=w_scales[:], in_=w_grouped[:])
+
+        def group_weight(copy, raw, first_col, passes):
+            cols = raw.shape[2] // 2
+            copy(
+                out=w_grouped_view[:, passes, first_col : first_col + cols, :],
+                in_=raw[:, 2 * passes.start : 2 * passes.stop, :].rearrange(
+                    "p (c u) (e n) -> p c n (u e)", u=2, e=2
+                ),
+            )
+
+        def quantise_weights(c):
+            words = slice(c * FEATURES, (c + 1) * FEATURES)
+            nc.vector.quantize_mx(
+                out=w_codes[:, words].bitcast(FP8X4),
+                scales=w_scales[:, words],
+                in_=w_grouped[:, 4 * words.start : 4 * words.stop],
+            )
+
+        zeros = const.tile([P, FEATURES], BF16, name="zeros")
+        nc.vector.memset(zeros[:], 0.0)
+
+        def keep_warm(count):
+            unread = psum_t.tile([P, WORDS], F32, name="x_t")
+            for m in range(count):
+                nc.tensor.matmul(
+                    unread[:], lhsT=zeros[:, :P], rhs=zeros[:], start=True, stop=True
+                )
+
+        def transpose_tile(j):
+            g, t = divmod(j, GROUP)
+            q, at = divmod(j, LOAD)
+            x_words = x_tiles[q][:, at * DIM : (at + 1) * DIM].bitcast(F32)
+            if t == 0:
+                grouped_tiles[g] = grouped_pool.tile(
+                    [P, GROUP * DIM], BF16, name="grouped", align_bytes=64
+                )
+            x_t = psum_t.tile([P, WORDS], F32, name="x_t")
+            for w in range(WORDS // P):
+                nc.tensor.transpose(
+                    x_t[:, w * P : (w + 1) * P], x_words[:, w * P : (w + 1) * P], ident[:]
+                )
+            nc.scalar.copy(
+                out=grouped_tiles[g][:].bitcast(F32)[:, t * WORDS : (t + 1) * WORDS].rearrange(
+                    "p (c r u) -> p c r u", c=PASSES, u=2
+                ),
+                in_=x_t[:].rearrange("p (c u r) -> p c r u", c=PASSES, u=2),
+            )
 
         def transpose_group(g):
-            q, half = divmod(g * GROUP, LOAD)
-            x_words = x_tiles[q][:, half * DIM : (half + GROUP) * DIM].bitcast(F32)
-            grouped = grouped_pool.tile([P, GROUP * DIM], BF16, name="grouped", align_bytes=64)
-            grouped_words = grouped[:].bitcast(F32)
-            for t in range(GROUP):
-                x_t = psum_t.tile([P, WORDS], F32, name="x_t")
-                for w in range(WORDS // P):
-                    first = t * WORDS + w * P
-                    nc.tensor.transpose(
-                        x_t[:, w * P : (w + 1) * P], x_words[:, first : first + P], ident[:]
-                    )
-                nc.scalar.copy(
-                    out=grouped_words[:, t * WORDS : (t + 1) * WORDS].rearrange(
-                        "p (c r u) -> p c r u", c=PASSES, u=2
-                    ),
-                    in_=x_t[:].rearrange("p (c u r) -> p c r u", c=PASSES, u=2),
+            for j in range(g * GROUP, (g + 1) * GROUP):
+                transpose_tile(j)
+
+        def quantise_group(g, first=0, last=GROUP):
+            if first == 0:
+                code_tiles[g] = mx_pool.tile(
+                    [P, GROUP * PASSES * P], U32, name="codes", align_bytes=64
                 )
-            grouped_tiles[g] = grouped
-
-        def quantise_group(g):
-            codes = mx_pool.tile([P, GROUP * PASSES * P], U32, name="codes", align_bytes=64)
-            scales = mx_pool.tile([P, GROUP * PASSES * P], U8, name="scales", align_bytes=64)
+                scale_tiles[g] = mx_pool.tile(
+                    [P, GROUP * PASSES * P], U8, name="scales", align_bytes=64
+                )
+            words = slice(first * PASSES * P, last * PASSES * P)
             nc.vector.quantize_mx(
-                out=codes[:].bitcast(FP8X4), scales=scales[:], in_=grouped_tiles[g][:]
+                out=code_tiles[g][:, words].bitcast(FP8X4),
+                scales=scale_tiles[g][:, words],
+                in_=grouped_tiles[g][:, first * DIM : last * DIM],
             )
-            code_tiles[g] = codes
-            scale_tiles[g] = scales
 
-        def multiply_group(g):
-            for t in range(GROUP):
+        def multiply_group(g, first=0, last=GROUP):
+            for t in range(first, last):
                 acc = psum_o.tile([P, FEATURES], F32, name="acc")
                 for c in range(PASSES):
                     tokens = slice((t * PASSES + c) * P, (t * PASSES + c + 1) * P)
@@ -186,7 +221,7 @@ def tile_attention_pa_t_kernel(tc, x, cos, sin, Wq, Wk, Wv, out_0, out_1, out_2)
                 for i in range(STORE // ROUND):
                     stage_tiles[r + i] = stage[:, :, i * ROUND : (i + 1) * ROUND, :]
                 store_tiles[r * ROUND // STORE] = stage
-            cross_tiles[r] = cross_pool.tile([P, ROTATED, ROUND, HEAD], F32, name="cross")
+            cross_tiles[r] = cross_pool.tile([P, ROUND, ROTATED, HEAD], F32, name="cross")
 
         def copy_v(r, t):
             nc.scalar.copy(
@@ -205,25 +240,33 @@ def tile_attention_pa_t_kernel(tc, x, cos, sin, Wq, Wk, Wv, out_0, out_1, out_2)
                 op=MULT,
             )
 
-        def sin_product(r, t):
+        def sin_product(r, t, first=0, last=ROTATED):
             j = (r * ROUND + t) % TILES_PER_BATCH
-            pairs = acc_tiles[r * ROUND + t][:, : ROTATED * HEAD].rearrange(
-                "p (h i e) -> p h i e", h=ROTATED, e=2
+            pairs = acc_tiles[r * ROUND + t][:, first * HEAD : last * HEAD].rearrange(
+                "p (h i e) -> p h i e", h=last - first, e=2
             )
             nc.vector.tensor_tensor(
-                out=cross_tiles[r][:, :, t, :].rearrange("p h (i e) -> p h i e", e=2),
+                out=cross_tiles[r][:, t, first:last, :].rearrange("p h (i e) -> p h i e", e=2),
                 in0=pairs[:, :, :, ::-1],
                 in1=sin_sb[:, j, :]
                 .rearrange("p (i e) -> p i e", e=2)
                 .unsqueeze(1)
-                .to_broadcast([P, ROTATED, PAIRS, 2]),
+                .to_broadcast([P, last - first, PAIRS, 2]),
                 op=MULT,
             )
 
         def add_partner(engine, r, tiles):
             rotated = stage_tiles[r][:, :ROTATED, tiles, :]
             engine.tensor_tensor(
-                out=rotated, in0=rotated, in1=cross_tiles[r][:, :, tiles, :], op=ADD
+                out=rotated, in0=rotated, in1=cross_tiles[r][:, tiles, :, :].rearrange("p s h d -> p h s d"), op=ADD
+            )
+
+        def store_v(first, count):
+            b, j0 = divmod(first, TILES_PER_BATCH)
+            s, t = divmod(first, STORE)
+            nc.sync.dma_start(
+                out=v_view[b, :, 0, j0 : j0 + count, :],
+                in_=store_tiles[s][:, ROTATED, t : t + count, :],
             )
 
         def store_tiles_of(first, count):
@@ -231,39 +274,67 @@ def tile_attention_pa_t_kernel(tc, x, cos, sin, Wq, Wk, Wv, out_0, out_1, out_2)
             rows = slice(j0, j0 + count)
             s, t = divmod(first, STORE)
             stage = store_tiles[s][:, :, t : t + count, :]
-            nc.sync.dma_start(out=v_view[b, :, 0, rows, :], in_=stage[:, 3, :, :])
             nc.sync.dma_start(out=q_view[b, :, :, rows, :], in_=stage[:, 0:2, :, :])
             nc.sync.dma_start(out=k_view[b, :, 0, rows, :], in_=stage[:, 2, :, :])
 
         LAST = ROUND - 1
-        for g in range(GROUPS_PER_ROUND):
-            transpose_group(g)
+        columns = (0, 2 * HEAD, 3 * HEAD)
+        both = slice(0, PASSES)
+        keep_warm(4)
+        transpose_tile(0)
+        for c in range(PASSES):
+            group_weight(nc.vector.tensor_copy, wq_raw, columns[0], slice(c, c + 1))
+        group_weight(nc.scalar.copy, wk_raw, columns[1], both)
+        quantise_group(0, 0, 1)
+        keep_warm(4)
+        transpose_tile(1)
+        group_weight(nc.vector.tensor_copy, wv_raw, columns[2], both)
+        keep_warm(2)
+        transpose_group(1)
+        for c in range(PASSES):
+            quantise_weights(c)
+        quantise_group(0, 1, 2)
+        multiply_group(0)
         sign_table(0)
-        for g in range(GROUPS_PER_ROUND):
-            quantise_group(g)
-            multiply_group(g)
+        quantise_group(1)
+        multiply_group(1)
         prepared = GROUPS_PER_ROUND
         for r in range(ROUNDS):
-            wanted = min(GROUPS, (r + 1 + AHEAD) * GROUPS_PER_ROUND)
+            wanted = min(GROUPS, (r + 1 + AHEAD) * GROUPS_PER_ROUND - (r == 0))
             due = range(prepared, wanted)
             prepared = wanted
             open_round(r)
             for t in range(ROUND):
                 copy_v(r, t)
+            if r + 4 >= ROUNDS:
+                store_v(r * ROUND, ROUND)
+            elif (r + 1) * ROUND % STORE == 0:
+                store_v((r + 1) * ROUND - STORE, STORE)
             for g in due:
                 transpose_group(g)
             if 0 < r < TABLE_PARTS:
                 sign_table(r)
             for t in range(ROUND):
+                if r + 1 == ROUNDS and t == 2:
+                    add_partner(nc.gpsimd, r, slice(0, 2))
+                    store_tiles_of(r * ROUND, 2)
                 cos_product(r, t)
                 if t < LAST:
                     sin_product(r, t)
+                else:
+                    sin_product(r, t, 0, ROTATED - 1)
             for g in due:
                 quantise_group(g)
-            add_partner(nc.vector, r, slice(0, VECTOR_ADDS))
-            sin_product(r, LAST)
-            add_partner(nc.gpsimd if r + 1 < ROUNDS else nc.vector, r, slice(VECTOR_ADDS, ROUND))
+            adds = VECTOR_ADDS if r + 2 < ROUNDS else 2
+            if r + 1 < ROUNDS:
+                add_partner(nc.vector, r, slice(0, adds))
+            sin_product(r, LAST, ROTATED - 1)
+            add_partner(nc.gpsimd if r + 1 < ROUNDS else nc.vector, r, slice(adds, ROUND))
             if r + 2 >= ROUNDS:
+                if r + 2 == ROUNDS:
+                    store_tiles_of(r * ROUND, 2)
+                store_tiles_of(r * ROUND + 2, 2)
+            elif r + 4 >= ROUNDS:
                 store_tiles_of(r * ROUND, ROUND)
             elif (r + 1) * ROUND % STORE == 0:
                 store_tiles_of((r + 1) * ROUND - STORE, STORE)

@@ -118,8 +118,8 @@ def tile_attention_pa_t_kernel(tc, x, cos, sin, Wq, Wk, Wv, out_0, out_1, out_2)
         wv_raw = load_weight(Wv, "wv_raw")
         load_x(GROUP, GROUP)
         load_tables(0)
-        for first in range(LOAD, 3 * LOAD, LOAD):
-            load_x(first, LOAD)
+        for first in range(LOAD, 3 * LOAD, GROUP):
+            load_x(first, GROUP)
         load_tables(1)
         for first in range(3 * LOAD, BATCH * TILES_PER_BATCH, LOAD):
             load_x(first, LOAD)
@@ -304,13 +304,19 @@ def tile_attention_pa_t_kernel(tc, x, cos, sin, Wq, Wk, Wv, out_0, out_1, out_2)
             due = range(prepared, wanted)
             prepared = wanted
             open_round(r)
-            for t in range(ROUND):
+            for t in range(GROUP if r > 0 else ROUND):
                 copy_v(r, t)
+            if r > 0:
+                for g in due[:1]:
+                    transpose_group(g)
+                multiply_group(r * GROUPS_PER_ROUND + 1)
+                for t in range(GROUP, ROUND):
+                    copy_v(r, t)
             if r + 4 >= ROUNDS:
                 store_v(r * ROUND, ROUND)
             elif (r + 1) * ROUND % STORE == 0:
                 store_v((r + 1) * ROUND - STORE, STORE)
-            for g in due:
+            for g in due[1:] if r > 0 else due:
                 transpose_group(g)
             if 0 < r < TABLE_PARTS:
                 sign_table(r)
@@ -339,5 +345,4 @@ def tile_attention_pa_t_kernel(tc, x, cos, sin, Wq, Wk, Wv, out_0, out_1, out_2)
             elif (r + 1) * ROUND % STORE == 0:
                 store_tiles_of((r + 1) * ROUND - STORE, STORE)
             if r + 1 < ROUNDS:
-                for g in range((r + 1) * GROUPS_PER_ROUND, (r + 2) * GROUPS_PER_ROUND):
-                    multiply_group(g)
+                multiply_group((r + 1) * GROUPS_PER_ROUND)

@@ -32,10 +32,10 @@ GROUPS_PER_ROUND = ROUND // GROUP
 LOAD = 4
 STORE = 8
 AHEAD = 2
-TABLE_PARTS = 2
+TABLE_PARTS = 4
 VECTOR_ADDS = 1
-T_BANKS = 3
-ACC_BANKS = 5
+T_BANKS = 4
+ACC_BANKS = 4
 
 FLOPS = 2 * BATCH * SEQ * DIM * FEATURES
 
@@ -118,9 +118,11 @@ def tile_attention_pa_t_kernel(tc, x, cos, sin, Wq, Wk, Wv, out_0, out_1, out_2)
         wv_raw = load_weight(Wv, "wv_raw")
         load_x(GROUP, GROUP)
         load_tables(0)
-        for first in range(LOAD, 3 * LOAD, GROUP):
-            load_x(first, GROUP)
-        load_tables(1)
+        for part in range(1, TABLE_PARTS - 1):
+            for first in range(part * LOAD, (part + 1) * LOAD, GROUP):
+                load_x(first, GROUP)
+            load_tables(part)
+        load_tables(TABLE_PARTS - 1)
         for first in range(3 * LOAD, BATCH * TILES_PER_BATCH, LOAD):
             load_x(first, LOAD)
 
@@ -291,6 +293,7 @@ def tile_attention_pa_t_kernel(tc, x, cos, sin, Wq, Wk, Wv, out_0, out_1, out_2)
         group_weight(nc.vector.tensor_copy, wv_raw, columns[2], both)
         keep_warm(2)
         transpose_group(1)
+        keep_warm(1)
         for c in range(PASSES):
             quantise_weights(c)
         quantise_group(0, 1, 2)
@@ -318,12 +321,11 @@ def tile_attention_pa_t_kernel(tc, x, cos, sin, Wq, Wk, Wv, out_0, out_1, out_2)
                 store_v((r + 1) * ROUND - STORE, STORE)
             for g in due[1:] if r > 0 else due:
                 transpose_group(g)
-            if 0 < r < TABLE_PARTS:
-                sign_table(r)
+            if r + 1 < TABLE_PARTS:
+                sign_table(r + 1)
             for t in range(ROUND):
-                if r + 1 == ROUNDS and t == 2:
-                    add_partner(nc.gpsimd, r, slice(0, 2))
-                    store_tiles_of(r * ROUND, 2)
+                if r + 1 == ROUNDS and t == 1:
+                    add_partner(nc.gpsimd, r, slice(0, 1))
                 cos_product(r, t)
                 if t < LAST:
                     sin_product(r, t)
@@ -335,6 +337,9 @@ def tile_attention_pa_t_kernel(tc, x, cos, sin, Wq, Wk, Wv, out_0, out_1, out_2)
             if r + 1 < ROUNDS:
                 add_partner(nc.vector, r, slice(0, adds))
             sin_product(r, LAST, ROTATED - 1)
+            if r + 1 == ROUNDS:
+                add_partner(nc.vector, r, slice(1, 2))
+                store_tiles_of(r * ROUND, 2)
             add_partner(nc.gpsimd if r + 1 < ROUNDS else nc.vector, r, slice(adds, ROUND))
             if r + 2 >= ROUNDS:
                 if r + 2 == ROUNDS:

@@ -33,7 +33,7 @@ LOAD = 4
 STORE = 8
 AHEAD = 2
 TABLE_PARTS = 4
-VECTOR_ADDS = 1
+VECTOR_FEATURES = 64
 T_BANKS = 4
 ACC_BANKS = 4
 
@@ -223,7 +223,7 @@ def tile_attention_pa_t_kernel(tc, x, cos, sin, Wq, Wk, Wv, out_0, out_1, out_2)
                 for i in range(STORE // ROUND):
                     stage_tiles[r + i] = stage[:, :, i * ROUND : (i + 1) * ROUND, :]
                 store_tiles[r * ROUND // STORE] = stage
-            cross_tiles[r] = cross_pool.tile([P, ROUND, ROTATED, HEAD], F32, name="cross")
+            cross_tiles[r] = cross_pool.tile([P, ROTATED, ROUND, HEAD], F32, name="cross")
 
         def copy_v(r, t):
             nc.scalar.copy(
@@ -248,7 +248,7 @@ def tile_attention_pa_t_kernel(tc, x, cos, sin, Wq, Wk, Wv, out_0, out_1, out_2)
                 "p (h i e) -> p h i e", h=last - first, e=2
             )
             nc.vector.tensor_tensor(
-                out=cross_tiles[r][:, t, first:last, :].rearrange("p h (i e) -> p h i e", e=2),
+                out=cross_tiles[r][:, first:last, t, :].rearrange("p h (i e) -> p h i e", e=2),
                 in0=pairs[:, :, :, ::-1],
                 in1=sin_sb[:, j, :]
                 .rearrange("p (i e) -> p i e", e=2)
@@ -258,10 +258,12 @@ def tile_attention_pa_t_kernel(tc, x, cos, sin, Wq, Wk, Wv, out_0, out_1, out_2)
             )
 
         def add_partner(engine, r, tiles):
-            rotated = stage_tiles[r][:, :ROTATED, tiles, :]
-            engine.tensor_tensor(
-                out=rotated, in0=rotated, in1=cross_tiles[r][:, tiles, :, :].rearrange("p s h d -> p h s d"), op=ADD
-            )
+            add_features(engine, r, tiles.start * HEAD, tiles.stop * HEAD)
+
+        def add_features(engine, r, first, last):
+            rotated = stage_tiles[r][:, :ROTATED].rearrange("p h t d -> p h (t d)")[:, :, first:last]
+            cross = cross_tiles[r][:].rearrange("p h t d -> p h (t d)")[:, :, first:last]
+            engine.tensor_tensor(out=rotated, in0=rotated, in1=cross, op=ADD)
 
         def store_v(first, count):
             b, j0 = divmod(first, TILES_PER_BATCH)
@@ -317,6 +319,10 @@ def tile_attention_pa_t_kernel(tc, x, cos, sin, Wq, Wk, Wv, out_0, out_1, out_2)
                     copy_v(r, t)
             if r + 4 >= ROUNDS:
                 store_v(r * ROUND, ROUND)
+                if r + 2 == ROUNDS:
+                    store_tiles_of((r - 1) * ROUND, 2)
+                elif r + 1 == ROUNDS:
+                    store_tiles_of((r - 1) * ROUND + 2, 2)
             elif (r + 1) * ROUND % STORE == 0:
                 store_v((r + 1) * ROUND - STORE, STORE)
             for g in due[1:] if r > 0 else due:
@@ -327,27 +333,33 @@ def tile_attention_pa_t_kernel(tc, x, cos, sin, Wq, Wk, Wv, out_0, out_1, out_2)
                 if r + 1 == ROUNDS and t == 1:
                     add_partner(nc.gpsimd, r, slice(0, 1))
                 cos_product(r, t)
-                if t < LAST:
-                    sin_product(r, t)
-                else:
-                    sin_product(r, t, 0, ROTATED - 1)
+                if r + 1 == ROUNDS and t == LAST:
+                    add_partner(nc.vector, r, slice(1, LAST))
+                sin_product(r, t, 0, ROTATED if t < LAST or r + 2 > ROUNDS else ROTATED - 1)
             for g in due:
                 quantise_group(g)
-            adds = VECTOR_ADDS if r + 2 < ROUNDS else 2
-            if r + 1 < ROUNDS:
-                add_partner(nc.vector, r, slice(0, adds))
-            sin_product(r, LAST, ROTATED - 1)
-            if r + 1 == ROUNDS:
-                add_partner(nc.vector, r, slice(1, 2))
+            if r + 2 < ROUNDS:
+                add_features(nc.vector, r, 0, VECTOR_FEATURES)
+                sin_product(r, LAST, ROTATED - 1)
+                if r + 3 < ROUNDS:
+                    add_features(nc.gpsimd, r, VECTOR_FEATURES, ROUND * HEAD)
+                else:
+                    add_partner(nc.gpsimd, r, slice(2, ROUND))
+                    store_tiles_of(r * ROUND + 2, 2)
+                    add_features(nc.gpsimd, r, VECTOR_FEATURES, 2 * HEAD)
+            elif r + 2 == ROUNDS:
+                add_partner(nc.vector, r, slice(0, 2))
                 store_tiles_of(r * ROUND, 2)
-            add_partner(nc.gpsimd if r + 1 < ROUNDS else nc.vector, r, slice(adds, ROUND))
-            if r + 2 >= ROUNDS:
-                if r + 2 == ROUNDS:
-                    store_tiles_of(r * ROUND, 2)
-                store_tiles_of(r * ROUND + 2, 2)
-            elif r + 4 >= ROUNDS:
+                sin_product(r, LAST, ROTATED - 1)
+                add_partner(nc.gpsimd, r, slice(2, ROUND))
+            else:
+                store_tiles_of(r * ROUND, 1)
+                store_tiles_of(r * ROUND + 1, LAST - 1)
+                add_partner(nc.vector, r, slice(LAST, ROUND))
+                store_tiles_of(r * ROUND + LAST, 1)
+            if r + 4 == ROUNDS:
                 store_tiles_of(r * ROUND, ROUND)
-            elif (r + 1) * ROUND % STORE == 0:
+            elif r + 4 < ROUNDS and (r + 1) * ROUND % STORE == 0:
                 store_tiles_of((r + 1) * ROUND - STORE, STORE)
             if r + 1 < ROUNDS:
                 multiply_group((r + 1) * GROUPS_PER_ROUND)

@@ -88,14 +88,11 @@ def tile_attention_pa_t_kernel(tc, x, cos, sin, Wq, Wk, Wv, out_0, out_1, out_2)
         cos_sb = const.tile([P, TILES_PER_BATCH, HEAD], BF16, name="cos_sb")
         sin_sb = const.tile([P, TILES_PER_BATCH, HEAD], BF16, name="sin_sb")
 
-        def load_tables(part):
-            tiles = slice(
-                part * TILES_PER_BATCH // TABLE_PARTS, (part + 1) * TILES_PER_BATCH // TABLE_PARTS
-            )
+        def load_tables(first, last):
             for table, table_sb in ((cos, cos_sb), (sin, sin_sb)):
                 nc.sync.dma_start(
-                    out=table_sb[:, tiles, :],
-                    in_=table.rearrange("(p j) d -> p j d", j=TILES_PER_BATCH)[:, tiles, :],
+                    out=table_sb[:, first:last, :],
+                    in_=table.rearrange("(p j) d -> p j d", j=TILES_PER_BATCH)[:, first:last, :],
                 )
 
         def sign_table(part):
@@ -116,15 +113,19 @@ def tile_attention_pa_t_kernel(tc, x, cos, sin, Wq, Wk, Wv, out_0, out_1, out_2)
         wk_raw = load_weight(Wk, "wk_raw")
         load_x(1, 1)
         wv_raw = load_weight(Wv, "wv_raw")
-        load_x(GROUP, GROUP)
-        load_tables(0)
-        for part in range(1, TABLE_PARTS - 1):
-            for first in range(part * LOAD, (part + 1) * LOAD, GROUP):
-                load_x(first, GROUP)
-            load_tables(part)
-        load_tables(TABLE_PARTS - 1)
-        for first in range(3 * LOAD, BATCH * TILES_PER_BATCH, LOAD):
-            load_x(first, LOAD)
+        load_x(2, 2)
+        load_tables(0, 4)
+        load_x(4, 2)
+        load_x(6, 2)
+        load_x(8, 2)
+        load_tables(4, 8)
+        load_x(10, 2)
+        load_x(12, 4)
+        load_tables(8, 16)
+        load_x(16, 4)
+        load_x(20, 4)
+        load_x(24, 4)
+        load_x(28, 4)
 
         ident = const.tile([P, P], F32, name="ident")
         make_identity(nc, ident[:])
@@ -290,12 +291,12 @@ def tile_attention_pa_t_kernel(tc, x, cos, sin, Wq, Wk, Wv, out_0, out_1, out_2)
             group_weight(nc.vector.tensor_copy, wq_raw, columns[0], slice(c, c + 1))
         group_weight(nc.scalar.copy, wk_raw, columns[1], both)
         quantise_group(0, 0, 1)
-        keep_warm(4)
+        keep_warm(6)
         transpose_tile(1)
         group_weight(nc.vector.tensor_copy, wv_raw, columns[2], both)
-        keep_warm(2)
+        keep_warm(4)
         transpose_group(1)
-        keep_warm(1)
+        keep_warm(2)
         for c in range(PASSES):
             quantise_weights(c)
         quantise_group(0, 1, 2)

@@ -31,7 +31,7 @@ ROUNDS = BATCH * TILES_PER_BATCH // ROUND
 GROUPS_PER_ROUND = ROUND // GROUP
 LOAD = 4
 STORE = 8
-AHEAD = 2
+AHEAD = 3
 TABLE_PARTS = 4
 VECTOR_FEATURES = 64
 T_BANKS = 4
@@ -261,9 +261,9 @@ def tile_attention_pa_t_kernel(tc, x, cos, sin, Wq, Wk, Wv, out_0, out_1, out_2)
         def add_partner(engine, r, tiles):
             add_features(engine, r, tiles.start * HEAD, tiles.stop * HEAD)
 
-        def add_features(engine, r, first, last):
-            rotated = stage_tiles[r][:, :ROTATED].rearrange("p h t d -> p h (t d)")[:, :, first:last]
-            cross = cross_tiles[r][:].rearrange("p h t d -> p h (t d)")[:, :, first:last]
+        def add_features(engine, r, first, last, heads=slice(0, ROTATED)):
+            rotated = stage_tiles[r][:, heads].rearrange("p h t d -> p h (t d)")[:, :, first:last]
+            cross = cross_tiles[r][:, heads].rearrange("p h t d -> p h (t d)")[:, :, first:last]
             engine.tensor_tensor(out=rotated, in0=rotated, in1=cross, op=ADD)
 
         def store_v(first, count):
@@ -274,13 +274,25 @@ def tile_attention_pa_t_kernel(tc, x, cos, sin, Wq, Wk, Wv, out_0, out_1, out_2)
                 in_=store_tiles[s][:, ROTATED, t : t + count, :],
             )
 
-        def store_tiles_of(first, count):
+        def store_q(first, count):
             b, j0 = divmod(first, TILES_PER_BATCH)
-            rows = slice(j0, j0 + count)
             s, t = divmod(first, STORE)
-            stage = store_tiles[s][:, :, t : t + count, :]
-            nc.sync.dma_start(out=q_view[b, :, :, rows, :], in_=stage[:, 0:2, :, :])
-            nc.sync.dma_start(out=k_view[b, :, 0, rows, :], in_=stage[:, 2, :, :])
+            nc.sync.dma_start(
+                out=q_view[b, :, :, j0 : j0 + count, :],
+                in_=store_tiles[s][:, 0:2, t : t + count, :],
+            )
+
+        def store_k(first, count):
+            b, j0 = divmod(first, TILES_PER_BATCH)
+            s, t = divmod(first, STORE)
+            nc.sync.dma_start(
+                out=k_view[b, :, 0, j0 : j0 + count, :],
+                in_=store_tiles[s][:, 2, t : t + count, :],
+            )
+
+        def store_tiles_of(first, count):
+            store_q(first, count)
+            store_k(first, count)
 
         LAST = ROUND - 1
         columns = (0, 2 * HEAD, 3 * HEAD)
@@ -306,7 +318,7 @@ def tile_attention_pa_t_kernel(tc, x, cos, sin, Wq, Wk, Wv, out_0, out_1, out_2)
         multiply_group(1)
         prepared = GROUPS_PER_ROUND
         for r in range(ROUNDS):
-            wanted = min(GROUPS, (r + 1 + AHEAD) * GROUPS_PER_ROUND - (r == 0))
+            wanted = min(GROUPS, (r + 1) * GROUPS_PER_ROUND + AHEAD)
             due = range(prepared, wanted)
             prepared = wanted
             open_round(r)
@@ -336,11 +348,12 @@ def tile_attention_pa_t_kernel(tc, x, cos, sin, Wq, Wk, Wv, out_0, out_1, out_2)
                 cos_product(r, t)
                 if r + 1 == ROUNDS and t == LAST:
                     add_partner(nc.vector, r, slice(1, LAST))
-                sin_product(r, t, 0, ROTATED if t < LAST or r + 2 > ROUNDS else ROTATED - 1)
+                sin_product(r, t, 0, ROTATED if t < LAST else ROTATED - 1)
             for g in due:
+                if g == due[-1] and r + 2 < ROUNDS:
+                    add_features(nc.vector, r, 0, VECTOR_FEATURES)
                 quantise_group(g)
             if r + 2 < ROUNDS:
-                add_features(nc.vector, r, 0, VECTOR_FEATURES)
                 sin_product(r, LAST, ROTATED - 1)
                 if r + 3 < ROUNDS:
                     add_features(nc.gpsimd, r, VECTOR_FEATURES, ROUND * HEAD)
@@ -356,8 +369,11 @@ def tile_attention_pa_t_kernel(tc, x, cos, sin, Wq, Wk, Wv, out_0, out_1, out_2)
             else:
                 store_tiles_of(r * ROUND, 1)
                 store_tiles_of(r * ROUND + 1, LAST - 1)
-                add_partner(nc.vector, r, slice(LAST, ROUND))
-                store_tiles_of(r * ROUND + LAST, 1)
+                sin_product(r, LAST, ROTATED - 1)
+                add_features(nc.vector, r, LAST * HEAD, ROUND * HEAD, slice(0, ROTATED - 1))
+                store_q(r * ROUND + LAST, 1)
+                add_features(nc.vector, r, LAST * HEAD, ROUND * HEAD, slice(ROTATED - 1, ROTATED))
+                store_k(r * ROUND + LAST, 1)
             if r + 4 == ROUNDS:
                 store_tiles_of(r * ROUND, ROUND)
             elif r + 4 < ROUNDS and (r + 1) * ROUND % STORE == 0:

@@ -113,7 +113,8 @@ def tile_attention_pa_t_kernel(tc, x, cos, sin, Wq, Wk, Wv, out_0, out_1, out_2)
         wk_raw = load_weight(Wk, "wk_raw")
         load_x(1, 1)
         wv_raw = load_weight(Wv, "wv_raw")
-        load_x(2, 2)
+        load_x(2, 1)
+        load_x(3, 1)
         load_tables(0, 4)
         load_x(4, 2)
         load_x(6, 2)
@@ -315,16 +316,23 @@ def tile_attention_pa_t_kernel(tc, x, cos, sin, Wq, Wk, Wv, out_0, out_1, out_2)
         multiply_group(0)
         sign_table(0)
         quantise_group(1)
-        multiply_group(1)
+        multiply_group(1, 0, 1)
+        open_round(0)
+        for t in range(LAST):
+            copy_v(0, t)
+        transpose_group(GROUPS_PER_ROUND)
+        multiply_group(1, 1, 2)
+        copy_v(0, LAST)
         prepared = GROUPS_PER_ROUND
         for r in range(ROUNDS):
             wanted = min(GROUPS, (r + 1) * GROUPS_PER_ROUND + AHEAD)
             due = range(prepared, wanted)
             prepared = wanted
-            open_round(r)
-            for t in range(GROUP if r > 0 else ROUND):
-                copy_v(r, t)
             if r > 0:
+                open_round(r)
+            if r > 0:
+                for t in range(GROUP):
+                    copy_v(r, t)
                 for g in due[:1]:
                     transpose_group(g)
                 multiply_group(r * GROUPS_PER_ROUND + 1)
@@ -338,7 +346,9 @@ def tile_attention_pa_t_kernel(tc, x, cos, sin, Wq, Wk, Wv, out_0, out_1, out_2)
                     store_tiles_of((r - 1) * ROUND + 2, 2)
             elif (r + 1) * ROUND % STORE == 0:
                 store_v((r + 1) * ROUND - STORE, STORE)
-            for g in due[1:] if r > 0 else due:
+            for g in due[1:]:
+                if r == 0 and g == due[-1]:
+                    keep_warm(2)
                 transpose_group(g)
             if r + 1 < TABLE_PARTS:
                 sign_table(r + 1)

@@ -33,7 +33,7 @@ LOAD = 4
 STORE = 8
 AHEAD = 3
 TABLE_PARTS = 4
-VECTOR_FEATURES = 64
+VECTOR_FEATURES = 72
 T_BANKS = 4
 ACC_BANKS = 4
 
@@ -145,8 +145,8 @@ def tile_attention_pa_t_kernel(tc, x, cos, sin, Wq, Wk, Wv, out_0, out_1, out_2)
                 ),
             )
 
-        def quantise_weights(c):
-            words = slice(c * FEATURES, (c + 1) * FEATURES)
+        def quantise_weights(c, first, last):
+            words = slice(c * FEATURES + first, c * FEATURES + last)
             nc.vector.quantize_mx(
                 out=w_codes[:, words].bitcast(FP8X4),
                 scales=w_scales[:, words],
@@ -267,6 +267,19 @@ def tile_attention_pa_t_kernel(tc, x, cos, sin, Wq, Wk, Wv, out_0, out_1, out_2)
             cross = cross_tiles[r][:, heads].rearrange("p h t d -> p h (t d)")[:, :, first:last]
             engine.tensor_tensor(out=rotated, in0=rotated, in1=cross, op=ADD)
 
+        def add_on_tensor(r, t):
+            total = psum_t.tile([P, WORDS], F32, name="x_t")
+            rotated = stage_tiles[r][:, :ROTATED, t, :]
+            for term in (rotated, cross_tiles[r][:, :, t, :]):
+                nc.tensor.matmul(
+                    total[:, : ROTATED * HEAD].rearrange("p (h d) -> p h d", h=ROTATED),
+                    lhsT=ident[:],
+                    rhs=term,
+                    start=(term is rotated),
+                    stop=(term is not rotated),
+                )
+            return total
+
         def store_v(first, count):
             b, j0 = divmod(first, TILES_PER_BATCH)
             s, t = divmod(first, STORE)
@@ -304,15 +317,17 @@ def tile_attention_pa_t_kernel(tc, x, cos, sin, Wq, Wk, Wv, out_0, out_1, out_2)
             group_weight(nc.vector.tensor_copy, wq_raw, columns[0], slice(c, c + 1))
         group_weight(nc.scalar.copy, wk_raw, columns[1], both)
         quantise_group(0, 0, 1)
-        keep_warm(6)
+        for c in range(PASSES):
+            quantise_weights(c, 0, 2 * HEAD)
+        keep_warm(4)
         transpose_tile(1)
         group_weight(nc.vector.tensor_copy, wv_raw, columns[2], both)
         keep_warm(4)
         transpose_group(1)
-        keep_warm(2)
-        for c in range(PASSES):
-            quantise_weights(c)
+        keep_warm(1)
         quantise_group(0, 1, 2)
+        for c in range(PASSES):
+            quantise_weights(c, 2 * HEAD, FEATURES)
         multiply_group(0)
         sign_table(0)
         quantise_group(1)
@@ -333,6 +348,12 @@ def tile_attention_pa_t_kernel(tc, x, cos, sin, Wq, Wk, Wv, out_0, out_1, out_2)
             if r > 0:
                 for t in range(GROUP):
                     copy_v(r, t)
+                if r + 1 == ROUNDS:
+                    nc.scalar.copy(
+                        out=stage_tiles[r - 1][:, :ROTATED, 0, :],
+                        in_=total[:, : ROTATED * HEAD].rearrange("p (h d) -> p h d", h=ROTATED),
+                    )
+                    store_tiles_of((r - 1) * ROUND, 2)
                 for g in due[:1]:
                     transpose_group(g)
                 multiply_group(r * GROUPS_PER_ROUND + 1)
@@ -354,10 +375,16 @@ def tile_attention_pa_t_kernel(tc, x, cos, sin, Wq, Wk, Wv, out_0, out_1, out_2)
                 sign_table(r + 1)
             for t in range(ROUND):
                 if r + 1 == ROUNDS and t == 1:
-                    add_partner(nc.gpsimd, r, slice(0, 1))
+                    total = add_on_tensor(r, 0)
+                    nc.scalar.copy(
+                        out=stage_tiles[r][:, :ROTATED, 0, :],
+                        in_=total[:, : ROTATED * HEAD].rearrange("p (h d) -> p h d", h=ROTATED),
+                    )
+                if r + 1 == ROUNDS and t == 2:
+                    add_partner(nc.gpsimd, r, slice(1, 2))
                 cos_product(r, t)
                 if r + 1 == ROUNDS and t == LAST:
-                    add_partner(nc.vector, r, slice(1, LAST))
+                    add_partner(nc.vector, r, slice(2, LAST))
                 sin_product(r, t, 0, ROTATED if t < LAST else ROTATED - 1)
             for g in due:
                 if g == due[-1] and r + 2 < ROUNDS:
@@ -372,13 +399,12 @@ def tile_attention_pa_t_kernel(tc, x, cos, sin, Wq, Wk, Wv, out_0, out_1, out_2)
                     store_tiles_of(r * ROUND + 2, 2)
                     add_features(nc.gpsimd, r, VECTOR_FEATURES, 2 * HEAD)
             elif r + 2 == ROUNDS:
-                add_partner(nc.vector, r, slice(0, 2))
-                store_tiles_of(r * ROUND, 2)
+                add_partner(nc.vector, r, slice(1, 2))
                 sin_product(r, LAST, ROTATED - 1)
                 add_partner(nc.gpsimd, r, slice(2, ROUND))
             else:
-                store_tiles_of(r * ROUND, 1)
-                store_tiles_of(r * ROUND + 1, LAST - 1)
+                store_tiles_of(r * ROUND, 2)
+                store_tiles_of(r * ROUND + 2, 1)
                 sin_product(r, LAST, ROTATED - 1)
                 add_features(nc.vector, r, LAST * HEAD, ROUND * HEAD, slice(0, ROTATED - 1))
                 store_q(r * ROUND + LAST, 1)
@@ -390,3 +416,5 @@ def tile_attention_pa_t_kernel(tc, x, cos, sin, Wq, Wk, Wv, out_0, out_1, out_2)
                 store_tiles_of((r + 1) * ROUND - STORE, STORE)
             if r + 1 < ROUNDS:
                 multiply_group((r + 1) * GROUPS_PER_ROUND)
+            if r + 2 == ROUNDS:
+                total = add_on_tensor(r, 0)

@@ -33,6 +33,7 @@ LOAD = 4
 STORE = 8
 AHEAD = 3
 TABLE_PARTS = 4
+TENSOR_ADDS = 2
 VECTOR_FEATURES = 72
 T_BANKS = 4
 ACC_BANKS = 4
@@ -267,18 +268,14 @@ def tile_attention_pa_t_kernel(tc, x, cos, sin, Wq, Wk, Wv, out_0, out_1, out_2)
             cross = cross_tiles[r][:, heads].rearrange("p h t d -> p h (t d)")[:, :, first:last]
             engine.tensor_tensor(out=rotated, in0=rotated, in1=cross, op=ADD)
 
-        def add_on_tensor(r, t):
+        def add_on_tensor(r, last):
             total = psum_t.tile([P, WORDS], F32, name="x_t")
-            rotated = stage_tiles[r][:, :ROTATED, t, :]
-            for term in (rotated, cross_tiles[r][:, :, t, :]):
-                nc.tensor.matmul(
-                    total[:, : ROTATED * HEAD].rearrange("p (h d) -> p h d", h=ROTATED),
-                    lhsT=ident[:],
-                    rhs=term,
-                    start=(term is rotated),
-                    stop=(term is not rotated),
-                )
-            return total
+            total_heads = total[:, : ROTATED * last].rearrange("p (h f) -> p h f", h=ROTATED)
+            rotated = stage_tiles[r][:, :ROTATED].rearrange("p h t d -> p h (t d)")[:, :, :last]
+            cross = cross_tiles[r][:].rearrange("p h t d -> p h (t d)")[:, :, :last]
+            nc.tensor.matmul(total_heads, lhsT=ident[:], rhs=rotated, start=True, stop=False)
+            nc.tensor.matmul(total_heads, lhsT=ident[:], rhs=cross, start=False, stop=True)
+            nc.scalar.copy(out=rotated, in_=total_heads)
 
         def store_v(first, count):
             b, j0 = divmod(first, TILES_PER_BATCH)
@@ -348,12 +345,6 @@ def tile_attention_pa_t_kernel(tc, x, cos, sin, Wq, Wk, Wv, out_0, out_1, out_2)
             if r > 0:
                 for t in range(GROUP):
                     copy_v(r, t)
-                if r + 1 == ROUNDS:
-                    nc.scalar.copy(
-                        out=stage_tiles[r - 1][:, :ROTATED, 0, :],
-                        in_=total[:, : ROTATED * HEAD].rearrange("p (h d) -> p h d", h=ROTATED),
-                    )
-                    store_tiles_of((r - 1) * ROUND, 2)
                 for g in due[:1]:
                     transpose_group(g)
                 multiply_group(r * GROUPS_PER_ROUND + 1)
@@ -375,11 +366,7 @@ def tile_attention_pa_t_kernel(tc, x, cos, sin, Wq, Wk, Wv, out_0, out_1, out_2)
                 sign_table(r + 1)
             for t in range(ROUND):
                 if r + 1 == ROUNDS and t == 1:
-                    total = add_on_tensor(r, 0)
-                    nc.scalar.copy(
-                        out=stage_tiles[r][:, :ROTATED, 0, :],
-                        in_=total[:, : ROTATED * HEAD].rearrange("p (h d) -> p h d", h=ROTATED),
-                    )
+                    add_on_tensor(r, HEAD)
                 if r + 1 == ROUNDS and t == 2:
                     add_partner(nc.gpsimd, r, slice(1, 2))
                 cos_product(r, t)
@@ -387,9 +374,13 @@ def tile_attention_pa_t_kernel(tc, x, cos, sin, Wq, Wk, Wv, out_0, out_1, out_2)
                     add_partner(nc.vector, r, slice(2, LAST))
                 sin_product(r, t, 0, ROTATED if t < LAST else ROTATED - 1)
             for g in due:
-                if g == due[-1] and r + 2 < ROUNDS:
+                if g == due[-1] and r + 2 < ROUNDS and r not in (2, 3, 4):
                     add_features(nc.vector, r, 0, VECTOR_FEATURES)
                 quantise_group(g)
+            if r in (2, 3, 4) or r + 2 == ROUNDS:
+                add_on_tensor(r, VECTOR_FEATURES if r + 2 < ROUNDS else HEAD)
+            if r + 1 < ROUNDS:
+                multiply_group((r + 1) * GROUPS_PER_ROUND)
             if r + 2 < ROUNDS:
                 sin_product(r, LAST, ROTATED - 1)
                 if r + 3 < ROUNDS:
@@ -400,6 +391,7 @@ def tile_attention_pa_t_kernel(tc, x, cos, sin, Wq, Wk, Wv, out_0, out_1, out_2)
                     add_features(nc.gpsimd, r, VECTOR_FEATURES, 2 * HEAD)
             elif r + 2 == ROUNDS:
                 add_partner(nc.vector, r, slice(1, 2))
+                store_tiles_of(r * ROUND, 2)
                 sin_product(r, LAST, ROTATED - 1)
                 add_partner(nc.gpsimd, r, slice(2, ROUND))
             else:
@@ -414,7 +406,3 @@ def tile_attention_pa_t_kernel(tc, x, cos, sin, Wq, Wk, Wv, out_0, out_1, out_2)
                 store_tiles_of(r * ROUND, ROUND)
             elif r + 4 < ROUNDS and (r + 1) * ROUND % STORE == 0:
                 store_tiles_of((r + 1) * ROUND - STORE, STORE)
-            if r + 1 < ROUNDS:
-                multiply_group((r + 1) * GROUPS_PER_ROUND)
-            if r + 2 == ROUNDS:
-                total = add_on_tensor(r, 0)

from contextlib import ExitStack

import concourse.mybir as mybir
from concourse.masks import make_identity

F32 = mybir.dt.float32
BF16 = mybir.dt.bfloat16
U32 = mybir.dt.uint32
U8 = mybir.dt.uint8
FP8X4 = mybir.dt.float8_e4m3fn_x4
MULT = mybir.AluOpType.mult
ADD = mybir.AluOpType.add
COPY = mybir.ActivationFunctionType.Copy

P = 128
BATCH = 2
SEQ = 2048
DIM = 1024
HEAD = 128
ROTATED = 3
FEATURES = 4 * HEAD
PAIRS = HEAD // 2
K_PASS = 4 * P
PASSES = DIM // K_PASS
WORDS = DIM // 2
TILES_PER_BATCH = SEQ // P
GROUP = 2
GROUPS = BATCH * TILES_PER_BATCH // GROUP
ROUND = 4
ROUNDS = BATCH * TILES_PER_BATCH // ROUND
GROUPS_PER_ROUND = ROUND // GROUP
LOAD = 4
STORE = 8
AHEAD = 3
TABLE_PARTS = 4
TENSOR_ADDS = 2
VECTOR_FEATURES = 72
T_BANKS = 4
ACC_BANKS = 4

FLOPS = 2 * BATCH * SEQ * DIM * FEATURES


def tile_attention_pa_t_kernel(tc, x, cos, sin, Wq, Wk, Wv, out_0, out_1, out_2):
    nc = tc.nc
    x_view = x.rearrange("b (p j) k -> b p j k", j=TILES_PER_BATCH)
    q_view = out_0.rearrange("b h (p j) d -> b p h j d", j=TILES_PER_BATCH)
    k_view = out_1.rearrange("b h (p j) d -> b p h j d", j=TILES_PER_BATCH)
    v_view = out_2.rearrange("b h (p j) d -> b p h j d", j=TILES_PER_BATCH)

    with ExitStack() as ctx:
        const = ctx.enter_context(tc.tile_pool(name="const", bufs=1))
        x_pool = ctx.enter_context(tc.tile_pool(name="x_pool", bufs=BATCH * TILES_PER_BATCH // LOAD))
        grouped_pool = ctx.enter_context(tc.tile_pool(name="grouped_pool", bufs=4))
        mx_pool = ctx.enter_context(tc.tile_pool(name="mx_pool", bufs=3 * GROUPS_PER_ROUND))
        cross_pool = ctx.enter_context(tc.tile_pool(name="cross_pool", bufs=3))
        stage_pool = ctx.enter_context(tc.tile_pool(name="stage_pool", bufs=4))
        psum_t = ctx.enter_context(tc.psum_pool(name="psum_t", bufs=T_BANKS))
        psum_o = ctx.enter_context(tc.psum_pool(name="psum_o", bufs=ACC_BANKS))
        ctx.enter_context(tc.manual_schedule())

        x_tiles = {}
        grouped_tiles = {}
        code_tiles = {}
        scale_tiles = {}
        acc_tiles = {}
        stage_tiles = {}
        store_tiles = {}
        cross_tiles = {}

        def load_x(first, count):
            q, t = divmod(first, LOAD)
            b, j0 = divmod(first, TILES_PER_BATCH)
            if t == 0:
                x_tiles[q] = x_pool.tile([P, LOAD * DIM], BF16, name="x_sb")
            nc.sync.dma_start(
                out=x_tiles[q][:, t * DIM : (t + count) * DIM],
                in_=x_view[b, :, j0 : j0 + count, :].rearrange("p j k -> p (j k)"),
            )

        def load_weight(w, name):
            cols = w.shape[1]
            raw = const.tile([P, 2 * PASSES, 2 * cols], BF16, name=name)
            nc.sync.dma_start(
                out=raw[:], in_=w.rearrange("(cu p e) n -> p cu (e n)", p=P, e=2)
            )
            return raw

        cos_sb = const.tile([P, TILES_PER_BATCH, HEAD], BF16, name="cos_sb")
        sin_sb = const.tile([P, TILES_PER_BATCH, HEAD], BF16, name="sin_sb")

        def load_tables(first, last):
            for table, table_sb in ((cos, cos_sb), (sin, sin_sb)):
                nc.sync.dma_start(
                    out=table_sb[:, first:last, :],
                    in_=table.rearrange("(p j) d -> p j d", j=TILES_PER_BATCH)[:, first:last, :],
                )

        def sign_table(part):
            tiles = slice(
                part * TILES_PER_BATCH // TABLE_PARTS, (part + 1) * TILES_PER_BATCH // TABLE_PARTS
            )
            even = sin_sb[:, tiles, :].rearrange("p j (i e) -> p j i e", e=2)[:, :, :, 0]
            nc.scalar.activation(out=even, in_=even, func=COPY, scale=-1.0)

        load_x(0, 1)
        wq_raw = const.tile([P, 2 * PASSES, 2 * Wq.shape[1]], BF16, name="wq_raw")
        for c in range(PASSES):
            halves = slice(2 * c, 2 * c + 2)
            nc.sync.dma_start(
                out=wq_raw[:, halves, :],
                in_=Wq.rearrange("(cu p e) n -> p cu (e n)", p=P, e=2)[:, halves, :],
            )
        wk_raw = load_weight(Wk, "wk_raw")
        load_x(1, 1)
        wv_raw = load_weight(Wv, "wv_raw")
        load_x(2, 1)
        load_x(3, 1)
        load_tables(0, 4)
        load_x(4, 2)
        load_x(6, 2)
        load_x(8, 2)
        load_tables(4, 8)
        load_x(10, 2)
        load_x(12, 4)
        load_tables(8, 16)
        load_x(16, 4)
        load_x(20, 4)
        load_x(24, 4)
        load_x(28, 4)

        ident = const.tile([P, P], F32, name="ident")
        make_identity(nc, ident[:])

        w_grouped = const.tile([P, PASSES * FEATURES * 4], BF16, name="w_grouped", align_bytes=64)
        w_grouped_view = w_grouped[:].rearrange("p (c n t) -> p c n t", c=PASSES, t=4)
        w_codes = const.tile([P, PASSES * FEATURES], U32, name="w_codes", align_bytes=64)
        w_scales = const.tile([P, PASSES * FEATURES], U8, name="w_scales", align_bytes=64)

        def group_weight(copy, raw, first_col, passes):
            cols = raw.shape[2] // 2
            copy(
                out=w_grouped_view[:, passes, first_col : first_col + cols, :],
                in_=raw[:, 2 * passes.start : 2 * passes.stop, :].rearrange(
                    "p (c u) (e n) -> p c n (u e)", u=2, e=2
                ),
            )

        def quantise_weights(c, first, last):
            words = slice(c * FEATURES + first, c * FEATURES + last)
            nc.vector.quantize_mx(
                out=w_codes[:, words].bitcast(FP8X4),
                scales=w_scales[:, words],
                in_=w_grouped[:, 4 * words.start : 4 * words.stop],
            )

        zeros = const.tile([P, FEATURES], BF16, name="zeros")
        nc.vector.memset(zeros[:], 0.0)

        def keep_warm(count):
            unread = psum_t.tile([P, WORDS], F32, name="x_t")
            for m in range(count):
                nc.tensor.matmul(
                    unread[:], lhsT=zeros[:, :P], rhs=zeros[:], start=True, stop=True
                )

        def transpose_tile(j):
            g, t = divmod(j, GROUP)
            q, at = divmod(j, LOAD)
            x_words = x_tiles[q][:, at * DIM : (at + 1) * DIM].bitcast(F32)
            if t == 0:
                grouped_tiles[g] = grouped_pool.tile(
                    [P, GROUP * DIM], BF16, name="grouped", align_bytes=64
                )
            x_t = psum_t.tile([P, WORDS], F32, name="x_t")
            for w in range(WORDS // P):
                nc.tensor.transpose(
                    x_t[:, w * P : (w + 1) * P], x_words[:, w * P : (w + 1) * P], ident[:]
                )
            nc.scalar.copy(
                out=grouped_tiles[g][:].bitcast(F32)[:, t * WORDS : (t + 1) * WORDS].rearrange(
                    "p (c r u) -> p c r u", c=PASSES, u=2
                ),
                in_=x_t[:].rearrange("p (c u r) -> p c r u", c=PASSES, u=2),
            )

        def transpose_group(g):
            for j in range(g * GROUP, (g + 1) * GROUP):
                transpose_tile(j)

        def quantise_group(g, first=0, last=GROUP):
            if first == 0:
                code_tiles[g] = mx_pool.tile(
                    [P, GROUP * PASSES * P], U32, name="codes", align_bytes=64
                )
                scale_tiles[g] = mx_pool.tile(
                    [P, GROUP * PASSES * P], U8, name="scales", align_bytes=64
                )
            words = slice(first * PASSES * P, last * PASSES * P)
            nc.vector.quantize_mx(
                out=code_tiles[g][:, words].bitcast(FP8X4),
                scales=scale_tiles[g][:, words],
                in_=grouped_tiles[g][:, first * DIM : last * DIM],
            )

        def multiply_group(g, first=0, last=GROUP):
            for t in range(first, last):
                acc = psum_o.tile([P, FEATURES], F32, name="acc")
                for c in range(PASSES):
                    tokens = slice((t * PASSES + c) * P, (t * PASSES + c + 1) * P)
                    features = slice(c * FEATURES, (c + 1) * FEATURES)
                    nc.tensor.matmul_mx(
                        out=acc[:],
                        lhsT=code_tiles[g][:, tokens].bitcast(FP8X4),
                        lhsT_scale=scale_tiles[g][:, tokens],
                        rhs=w_codes[:, features].bitcast(FP8X4),
                        rhs_scale=w_scales[:, features],
                        start=(c == 0),
                        stop=(c == PASSES - 1),
                    )
                acc_tiles[g * GROUP + t] = acc

        def open_round(r):
            if r * ROUND % STORE == 0:
                stage = stage_pool.tile([P, 4, STORE, HEAD], F32, name="stage")
                for i in range(STORE // ROUND):
                    stage_tiles[r + i] = stage[:, :, i * ROUND : (i + 1) * ROUND, :]
                store_tiles[r * ROUND // STORE] = stage
            cross_tiles[r] = cross_pool.tile([P, ROTATED, ROUND, HEAD], F32, name="cross")

        def copy_v(r, t):
            nc.scalar.copy(
                out=stage_tiles[r][:, ROTATED, t, :],
                in_=acc_tiles[r * ROUND + t][:, ROTATED * HEAD :],
            )

        def cos_product(r, t):
            j = (r * ROUND + t) % TILES_PER_BATCH
            nc.vector.tensor_tensor(
                out=stage_tiles[r][:, :ROTATED, t, :],
                in0=acc_tiles[r * ROUND + t][:, : ROTATED * HEAD].rearrange(
                    "p (h d) -> p h d", h=ROTATED
                ),
                in1=cos_sb[:, j, :].unsqueeze(1).to_broadcast([P, ROTATED, HEAD]),
                op=MULT,
            )

        def sin_product(r, t, first=0, last=ROTATED):
            j = (r * ROUND + t) % TILES_PER_BATCH
            pairs = acc_tiles[r * ROUND + t][:, first * HEAD : last * HEAD].rearrange(
                "p (h i e) -> p h i e", h=last - first, e=2
            )
            nc.vector.tensor_tensor(
                out=cross_tiles[r][:, first:last, t, :].rearrange("p h (i e) -> p h i e", e=2),
                in0=pairs[:, :, :, ::-1],
                in1=sin_sb[:, j, :]
                .rearrange("p (i e) -> p i e", e=2)
                .unsqueeze(1)
                .to_broadcast([P, last - first, PAIRS, 2]),
                op=MULT,
            )

        def add_partner(engine, r, tiles):
            add_features(engine, r, tiles.start * HEAD, tiles.stop * HEAD)

        def add_features(engine, r, first, last, heads=slice(0, ROTATED)):
            rotated = stage_tiles[r][:, heads].rearrange("p h t d -> p h (t d)")[:, :, first:last]
            cross = cross_tiles[r][:, heads].rearrange("p h t d -> p h (t d)")[:, :, first:last]
            engine.tensor_tensor(out=rotated, in0=rotated, in1=cross, op=ADD)

        def add_on_tensor(r, last):
            total = psum_t.tile([P, WORDS], F32, name="x_t")
            total_heads = total[:, : ROTATED * last].rearrange("p (h f) -> p h f", h=ROTATED)
            rotated = stage_tiles[r][:, :ROTATED].rearrange("p h t d -> p h (t d)")[:, :, :last]
            cross = cross_tiles[r][:].rearrange("p h t d -> p h (t d)")[:, :, :last]
            nc.tensor.matmul(total_heads, lhsT=ident[:], rhs=rotated, start=True, stop=False)
            nc.tensor.matmul(total_heads, lhsT=ident[:], rhs=cross, start=False, stop=True)
            nc.scalar.copy(out=rotated, in_=total_heads)

        def store_v(first, count):
            b, j0 = divmod(first, TILES_PER_BATCH)
            s, t = divmod(first, STORE)
            nc.sync.dma_start(
                out=v_view[b, :, 0, j0 : j0 + count, :],
                in_=store_tiles[s][:, ROTATED, t : t + count, :],
            )

        def store_q(first, count):
            b, j0 = divmod(first, TILES_PER_BATCH)
            s, t = divmod(first, STORE)
            nc.sync.dma_start(
                out=q_view[b, :, :, j0 : j0 + count, :],
                in_=store_tiles[s][:, 0:2, t : t + count, :],
            )

        def store_k(first, count):
            b, j0 = divmod(first, TILES_PER_BATCH)
            s, t = divmod(first, STORE)
            nc.sync.dma_start(
                out=k_view[b, :, 0, j0 : j0 + count, :],
                in_=store_tiles[s][:, 2, t : t + count, :],
            )

        def store_tiles_of(first, count):
            store_q(first, count)
            store_k(first, count)

        LAST = ROUND - 1
        columns = (0, 2 * HEAD, 3 * HEAD)
        both = slice(0, PASSES)
        keep_warm(4)
        transpose_tile(0)
        for c in range(PASSES):
            group_weight(nc.vector.tensor_copy, wq_raw, columns[0], slice(c, c + 1))
        group_weight(nc.scalar.copy, wk_raw, columns[1], both)
        quantise_group(0, 0, 1)
        for c in range(PASSES):
            quantise_weights(c, 0, 2 * HEAD)
        keep_warm(4)
        transpose_tile(1)
        group_weight(nc.vector.tensor_copy, wv_raw, columns[2], both)
        keep_warm(4)
        transpose_group(1)
        keep_warm(1)
        quantise_group(0, 1, 2)
        for c in range(PASSES):
            quantise_weights(c, 2 * HEAD, FEATURES)
        multiply_group(0)
        sign_table(0)
        quantise_group(1)
        multiply_group(1, 0, 1)
        open_round(0)
        for t in range(LAST):
            copy_v(0, t)
        transpose_group(GROUPS_PER_ROUND)
        multiply_group(1, 1, 2)
        copy_v(0, LAST)
        prepared = GROUPS_PER_ROUND
        for r in range(ROUNDS):
            wanted = min(GROUPS, (r + 1) * GROUPS_PER_ROUND + AHEAD)
            due = range(prepared, wanted)
            prepared = wanted
            if r > 0:
                open_round(r)
            if r > 0:
                for t in range(GROUP):
                    copy_v(r, t)
                for g in due[:1]:
                    transpose_group(g)
                multiply_group(r * GROUPS_PER_ROUND + 1)
                for t in range(GROUP, ROUND):
                    copy_v(r, t)
            if r + 4 >= ROUNDS:
                store_v(r * ROUND, ROUND)
                if r + 2 == ROUNDS:
                    store_tiles_of((r - 1) * ROUND, 2)
                elif r + 1 == ROUNDS:
                    store_tiles_of((r - 1) * ROUND + 2, 2)
            elif (r + 1) * ROUND % STORE == 0:
                store_v((r + 1) * ROUND - STORE, STORE)
            for g in due[1:]:
                if r == 0 and g == due[-1]:
                    keep_warm(2)
                transpose_group(g)
            if r + 1 < TABLE_PARTS:
                sign_table(r + 1)
            for t in range(ROUND):
                if r + 1 == ROUNDS and t == 1:
                    add_on_tensor(r, HEAD)
                if r + 1 == ROUNDS and t == 2:
                    add_partner(nc.gpsimd, r, slice(1, 2))
                cos_product(r, t)
                if r + 1 == ROUNDS and t == LAST:
                    add_partner(nc.vector, r, slice(2, LAST))
                sin_product(r, t, 0, ROTATED if t < LAST else ROTATED - 1)
            for g in due:
                if g == due[-1] and r + 2 < ROUNDS and r not in (2, 3, 4):
                    add_features(nc.vector, r, 0, VECTOR_FEATURES)
                quantise_group(g)
            if r in (2, 3, 4) or r + 2 == ROUNDS:
                add_on_tensor(r, VECTOR_FEATURES if r + 2 < ROUNDS else HEAD)
            if r + 1 < ROUNDS:
                multiply_group((r + 1) * GROUPS_PER_ROUND)
            if r + 2 < ROUNDS:
                sin_product(r, LAST, ROTATED - 1)
                if r + 3 < ROUNDS:
                    add_features(nc.gpsimd, r, VECTOR_FEATURES, ROUND * HEAD)
                else:
                    add_partner(nc.gpsimd, r, slice(2, ROUND))
                    store_tiles_of(r * ROUND + 2, 2)
                    add_features(nc.gpsimd, r, VECTOR_FEATURES, 2 * HEAD)
            elif r + 2 == ROUNDS:
                add_partner(nc.vector, r, slice(1, 2))
                store_tiles_of(r * ROUND, 2)
                sin_product(r, LAST, ROTATED - 1)
                add_partner(nc.gpsimd, r, slice(2, ROUND))
            else:
                store_tiles_of(r * ROUND, 2)
                store_tiles_of(r * ROUND + 2, 1)
                sin_product(r, LAST, ROTATED - 1)
                add_features(nc.vector, r, LAST * HEAD, ROUND * HEAD, slice(0, ROTATED - 1))
                store_q(r * ROUND + LAST, 1)
                add_features(nc.vector, r, LAST * HEAD, ROUND * HEAD, slice(ROTATED - 1, ROTATED))
                store_k(r * ROUND + LAST, 1)
            if r + 4 == ROUNDS:
                store_tiles_of(r * ROUND, ROUND)
            elif r + 4 < ROUNDS and (r + 1) * ROUND % STORE == 0:
                store_tiles_of((r + 1) * ROUND - STORE, STORE)
